import numpy as np
import ml_dtypes


def mxq(x, axis, fmt="e4m3"):
    dtype, down = {"e4m3": (ml_dtypes.float8_e4m3fn, 7), "e5m2": (ml_dtypes.float8_e5m2, 14)}[fmt]
    v = np.moveaxis(np.asarray(x, np.float32).astype(ml_dtypes.bfloat16).astype(np.float64), axis, -1)
    blocks = v.reshape(v.shape[:-1] + (-1, 32))
    amax = np.abs(blocks).max(-1, keepdims=True)
    byte = np.maximum(np.where(amax > 0, np.frexp(amax)[1] - 1 + 127, 0) - down, 1)
    scale = np.exp2(byte - 127.0)
    codes = (blocks / scale).astype(np.float32).astype(dtype).astype(np.float64)
    return np.moveaxis((codes * scale).reshape(v.shape), -1, axis)


WIDE = False


def mx_kscale(k):
    if not WIDE:
        return np.ones(k)
    levels = np.array([10, -10, 5, -5, 0])
    if k % 512:
        return np.exp2(np.random.permutation(np.resize(levels, k // 32))).repeat(32)
    a = np.empty((k // 512, 16))
    for p in range(k // 512):
        a[p, :8] = np.random.permutation(np.resize(levels, 8))
        for g in range(8):
            far = levels[np.abs(levels - a[p, g]) >= 10]
            a[p, g + 8] = far[np.random.randint(len(far))]
    return np.exp2(a.ravel()).repeat(32)


BF16 = ml_dtypes.bfloat16


def bf(x):
    return np.asarray(x, np.float32).astype(BF16)


def f64(x):
    return np.asarray(x).astype(np.float64)


B, D, H, K = 5120, 1024, 1024, 128
EPS_B = 1e-8


def silu(v):
    return v / (1.0 + np.exp(-v))


def softplus(v):
    return np.maximum(v, 0.0) + np.log(1.0 + np.exp(-np.abs(v)))


def draw0():
    s = mx_kscale(H)
    return {"h_act": bf(silu(np.random.standard_normal((B, H))) * s),
            "W3": bf(np.random.standard_normal((H, K)) * 3.0 / np.sqrt(H) / s[:, None]),
            "b3": bf(0.5 * np.random.standard_normal(K))}


def core(h_act, W3, b3):
    logits = (mxq(f64(h_act), 1, "e4m3") @ mxq(f64(W3), 0, "e4m3")) + f64(b3)
    evidence = softplus(logits)
    alpha = evidence + 1.0
    S = alpha.sum(-1, keepdims=True)
    expected_prob = alpha / S
    vacuity = float(K) / S[:, 0]
    belief = evidence / S
    full = np.zeros(belief.shape[0])
    for i in range(K):
        bi = belief[:, i:i + 1]
        full = full + ((1.0 - np.abs(bi - belief) / (bi + belief + EPS_B)) * bi * belief).sum(-1)
    dissonance = 0.5 * (full - (belief * belief).sum(-1))
    return (alpha, evidence, expected_prob, vacuity, dissonance)


def e4m3fn_bytes(y):
    return np.clip(np.asarray(y, np.float64), -448.0, 448.0).astype(np.float32).astype(ml_dtypes.float8_e4m3fn).view(np.uint8)


def e4m3fn_values(b):
    return np.asarray(b, np.uint8).view(ml_dtypes.float8_e4m3fn).astype(np.float64)


def setup_inputs():
    d = draw0()
    x0 = np.asarray(d['h_act']).astype(np.float64)
    s = (np.max(np.abs(x0), axis=(0,), keepdims=True) / 448.0).astype(np.float32)
    out = {}
    for k, v in d.items():
        if k == 'h_act':
            out['h_act_bytes'] = e4m3fn_bytes(x0 / s.astype(np.float64))
            out['h_act_scale'] = s
        else:
            out[k] = v
    return out


def reference(h_act_bytes, h_act_scale, W3, b3):
    return core(e4m3fn_values(h_act_bytes) * h_act_scale.astype(np.float64), W3, b3)

@@ -1,0 +1,420 @@
+from contextlib import ExitStack
+
+import concourse.mybir as mybir
+from concourse.masks import make_identity
+
+ROWS, K, C = 5120, 1024, 128
+FLOPS = 2 * ROWS * K * C
+
+F32 = mybir.dt.float32
+BF16 = mybir.dt.bfloat16
+I32 = mybir.dt.int32
+U32 = mybir.dt.uint32
+U8 = mybir.dt.uint8
+FP8 = mybir.dt.float8_e4m3fn
+FP8X4 = mybir.dt.float8_e4m3fn_x4
+ACT = mybir.ActivationFunctionType
+ALU = mybir.AluOpType
+AX = mybir.AxisListType
+
+P = 128
+TILES = ROWS // P
+GROUP = 4
+GROUPS = TILES // GROUP
+PASSES = K // (4 * P)
+WORDS = 2 * P
+FIRST_LOAD = 2
+LEVELS = 7
+EPS = 1e-8
+PAIRS = C * (C - 1) // 2
+
+ROW_SPLIT = 72
+SUM_ROWS = 8
+
+CHAIN_SPAN = 0.95
+FEED_SPAN = 0.9
+SUM_SPAN = 0.9
+AFTER_TILE = 2500
+AFTER_STEP = 800
+
+
+def flat(ap):
+    return ap.rearrange("p t c -> p (t c)")
+
+
+def interleave(a, b):
+    out = []
+    for i in range(max(len(a), len(b))):
+        out.extend(a[i : i + 1])
+        out.extend(b[i : i + 1])
+    return out
+
+
+def tile_evidentialhead_pb_kernel(tc, h_act_bytes, h_act_scale, W3, b3, out_0, out_1, out_2, out_3, out_4):
+    nc = tc.nc
+    with ExitStack() as ctx:
+        ctx.enter_context(tc.manual_schedule())
+        const = ctx.enter_context(tc.tile_pool(name="const", bufs=1))
+        stage = ctx.enter_context(tc.tile_pool(name="stage", bufs=3))
+        grp = ctx.enter_context(tc.tile_pool(name="grp", bufs=2))
+        outp = ctx.enter_context(tc.tile_pool(name="outp", bufs=1))
+        sortp = ctx.enter_context(tc.tile_pool(name="sortp", bufs=3))
+        fin = ctx.enter_context(tc.tile_pool(name="fin", bufs=2))
+        psum_t = ctx.enter_context(tc.psum_pool(name="psum_t", bufs=2))
+        psum_acc = ctx.enter_context(tc.psum_pool(name="psum_acc", bufs=2))
+        psum_w = ctx.enter_context(tc.psum_pool(name="psum_w", bufs=2))
+        psum_wb = ctx.enter_context(tc.psum_pool(name="psum_wb", bufs=2))
+
+        bytes_hbm = h_act_bytes.rearrange("(p t) k -> p t k", t=TILES)
+        alpha_hbm = out_0.rearrange("(p t) c -> p t c", t=TILES)
+        evidence_hbm = out_1.rearrange("(p t) c -> p t c", t=TILES)
+        prob_hbm = out_2.rearrange("(p t) c -> p t c", t=TILES)
+        vacuity_hbm = out_3.rearrange("(p t) -> p t", t=TILES)
+        dissonance_hbm = out_4.rearrange("(p t) -> p t", t=TILES)
+
+        hbytes = const.tile([P, TILES, K], U8, name="hbytes")
+        scale_bc = const.tile([P, K], F32, name="scale_bc")
+        w_raw = const.tile([P, PASSES, 4, C], BF16, name="w_raw")
+        bias_bc = const.tile([P, C], BF16, name="bias_bc")
+        nc.scalar.dma_start(out=scale_bc[:], in_=h_act_scale.rearrange("o k -> (o k)").partition_broadcast(P))
+        nc.sync.dma_start(out=hbytes[:, 0:FIRST_LOAD, :], in_=bytes_hbm[:, 0:FIRST_LOAD, :])
+        nc.sync.dma_start(out=w_raw[:], in_=W3.rearrange("(q p j) n -> p q j n", p=P, j=4))
+        nc.sync.dma_start(out=bias_bc[:], in_=b3.partition_broadcast(P))
+        for t in range(FIRST_LOAD, TILES, GROUP):
+            e = min(t + GROUP, TILES)
+            nc.sync.dma_start(out=hbytes[:, t:e, :], in_=bytes_hbm[:, t:e, :])
+
+        zeros = const.tile([P, SUM_ROWS, P], F32, name="zeros")
+        nc.gpsimd.memset(zeros[:], 0.0)
+        ident = const.tile([P, P], F32, name="ident")
+        make_identity(nc, ident[:])
+        index_i = const.tile([P, C], I32, name="index_i")
+        nc.gpsimd.iota(out=index_i[:], pattern=[[1, C]], base=0, channel_multiplier=0)
+
+        warm = const.tile([P, 1], F32, name="warm")
+        nc.scalar.activation(out=warm[:], in_=zeros[:, 0, 0:1], func=ACT.Exp)
+
+        th_high = const.tile([P, P - ROW_SPLIT, P], F32, name="th_high")
+        th_low = [const.tile([P, ROW_SPLIT, ROW_SPLIT], F32, name="th_low0"), const.tile([P, ROW_SPLIT, ROW_SPLIT], F32, name="th_low1")]
+        row_sums = [const.tile([P, P], F32, name="row_sums0"), const.tile([P, P], F32, name="row_sums1")]
+        for a in range(0, ROW_SPLIT, SUM_ROWS):
+            for low in th_low:
+                nc.scalar.copy(out=low[:, a : a + SUM_ROWS, a:ROW_SPLIT], in_=zeros[:, :, a:ROW_SPLIT])
+        for sums_tile in row_sums:
+            nc.scalar.copy(out=sums_tile[:, ROW_SPLIT:P], in_=zeros[:, 0, ROW_SPLIT:P])
+        for a in range(ROW_SPLIT, P, SUM_ROWS):
+            nc.scalar.copy(out=th_high[:, a - ROW_SPLIT : a - ROW_SPLIT + SUM_ROWS, a:P], in_=zeros[:, :, a:P])
+
+        a_row = const.tile([P, C], F32, name="a_row")
+        nc.vector.tensor_copy(out=a_row[:], in_=index_i[:])
+        nc.vector.tensor_scalar(out=a_row[:, 0:ROW_SPLIT], in0=a_row[:, 0:ROW_SPLIT], scalar1=float(ROW_SPLIT - P), scalar2=None, op0=ALU.add)
+        nc.vector.tensor_scalar(out=a_row[:, ROW_SPLIT:P], in0=a_row[:, ROW_SPLIT:P], scalar1=float(-P), scalar2=None, op0=ALU.add)
+        eps_a = const.tile([P, GROUP, C], F32, name="eps_a")
+        for s in range(GROUP):
+            nc.vector.tensor_scalar(out=eps_a[:, s, :], in0=a_row[:], scalar1=EPS, scalar2=None, op0=ALU.mult)
+        one_col = const.tile([P, 1], F32, name="one_col")
+        nc.vector.memset(one_col[:], 1.0)
+        half_eps_col = const.tile([P, 1], F32, name="half_eps_col")
+        nc.vector.tensor_scalar(out=half_eps_col[:], in0=zeros[:, 0, 0:1], scalar1=0.5 * EPS, scalar2=None, op0=ALU.add)
+
+        w_grouped = const.tile([P, PASSES, C, 4], BF16, name="w_grouped", align_bytes=64)
+        nc.vector.tensor_copy(out=w_grouped[:], in_=w_raw[:].rearrange("p q j n -> p q n j"))
+        w_codes = const.tile([P, PASSES * C], U32, name="w_codes", align_bytes=64)
+        w_scales = const.tile([P, PASSES * C], U8, name="w_scales", align_bytes=64)
+        bias_grp = const.tile([P, GROUP, C], BF16, name="bias_grp")
+        for s in range(GROUP):
+            nc.vector.tensor_copy(out=bias_grp[:, s, :], in_=bias_bc[:])
+        nc.vector.quantize_mx(out=w_codes[:].bitcast(FP8X4), scales=w_scales[:], in_=w_grouped[:].rearrange("p q n j -> p (q n j)"))
+
+        vacuity = const.tile([P, TILES], F32, name="vacuity")
+        dissonance = const.tile([P, TILES], F32, name="dissonance")
+        weighted = const.tile([P, TILES], F32, name="weighted")
+        sum_low = const.tile([P, TILES], F32, name="sum_low")
+        sum_high = const.tile([P, TILES], F32, name="sum_high")
+
+        logit_of = [None] * GROUPS
+        soft_of = [None] * GROUPS
+        x_of = [None] * GROUPS
+        hneg_of = [None] * GROUPS
+
+        def stage_a(g):
+            turned_of, grouped_of, held = {}, {}, {}
+
+            def widen(s):
+                def unit():
+                    if s == 0:
+                        logit_of[g] = grp.tile([P, GROUP, C], F32, name="logit_g", tag="logit")
+                        soft_of[g] = grp.tile([P, GROUP, C], F32, name="soft_g", tag="soft")
+                    h_bf = stage.tile([P, K], BF16, name="h_bf", tag="h_bf", align_bytes=64)
+                    nc.vector.tensor_tensor(out=h_bf[:], in0=hbytes[:, GROUP * g + s, :].bitcast(FP8), in1=scale_bc[:], op=ALU.mult)
+                    words = h_bf[:].bitcast(F32)
+                    turned = psum_t.tile([P, PASSES, 2, P], F32, name="turned", tag="turned")
+                    for q in range(PASSES):
+                        for u in range(2):
+                            nc.tensor.transpose(turned[:, q, u, :], words[:, WORDS * q + u : WORDS * (q + 1) : 2], ident[:])
+                    turned_of[s] = turned
+
+                return unit
+
+            def copy_out(s):
+                def unit():
+                    grouped = stage.tile([P, PASSES, P, 4], BF16, name="grouped", tag="grouped", align_bytes=64)
+                    nc.vector.tensor_copy(out=grouped[:].bitcast(F32), in_=turned_of[s][:].rearrange("p q u r -> p q r u"))
+                    grouped_of[s] = grouped
+
+                return unit
+
+            def quantise(s):
+                def unit():
+                    codes = stage.tile([P, PASSES * P], U32, name="codes", tag="codes", align_bytes=64)
+                    scales = stage.tile([P, PASSES * P], U8, name="scales", tag="scales", align_bytes=64)
+                    nc.vector.quantize_mx(out=codes[:].bitcast(FP8X4), scales=scales[:], in_=grouped_of[s][:].rearrange("p q r t -> p (q r t)"))
+                    if s == 0:
+                        held["acc"] = psum_acc.tile([P, GROUP, C], F32, name="acc", tag="acc")
+                    for q in range(PASSES):
+                        cols = slice(P * q, P * (q + 1))
+                        nc.tensor.matmul_mx(
+                            out=held["acc"][:, s, :],
+                            lhsT=codes[:, cols].bitcast(FP8X4),
+                            lhsT_scale=scales[:, cols],
+                            rhs=w_codes[:, cols].bitcast(FP8X4),
+                            rhs_scale=w_scales[:, cols],
+                            start=(q == 0),
+                            stop=(q == PASSES - 1),
+                        )
+
+                return unit
+
+            def add_bias():
+                nc.vector.tensor_tensor(out=logit_of[g][:], in0=held["acc"][:], in1=bias_grp[:], op=ALU.add)
+
+            def neg_abs():
+                v = flat(logit_of[g][:])
+                nc.vector.scalar_tensor_tensor(out=flat(soft_of[g][:]), in0=v, scalar=-1.0, in1=v, op0=ALU.mult, op1=ALU.min)
+
+            units = []
+            for s in range(GROUP + 2):
+                if s < GROUP:
+                    units.append(widen(s))
+                if 1 <= s <= GROUP:
+                    units.append(copy_out(s - 1))
+                if s >= 2:
+                    units.append(quantise(s - 2))
+            return units + [add_bias, neg_abs]
+
+        def stage_b(g):
+            tiles = slice(GROUP * g, GROUP * (g + 1))
+            held = {}
+
+            def evidence():
+                held["ev"] = outp.tile([P, GROUP, C], F32, name="ev_g", tag="ev")
+                nc.vector.scalar_tensor_tensor(out=flat(held["ev"][:]), in0=flat(logit_of[g][:]), scalar=0.0, in1=flat(soft_of[g][:]), op0=ALU.max, op1=ALU.add)
+                nc.sync.dma_start(out=evidence_hbm[:, tiles, :], in_=held["ev"][:])
+
+            def alpha():
+                held["al"] = outp.tile([P, GROUP, C], F32, name="al_g", tag="al")
+                nc.vector.tensor_scalar(out=flat(held["al"][:]), in0=flat(held["ev"][:]), scalar1=1.0, scalar2=None, op0=ALU.add)
+                nc.sync.dma_start(out=alpha_hbm[:, tiles, :], in_=held["al"][:])
+
+            def evidence_sum():
+                held["S"] = fin.tile([P, GROUP], F32, name="s_g", tag="S")
+                nc.vector.tensor_reduce(out=held["S"][:], in_=held["ev"][:], axis=AX.X, op=ALU.add)
+
+            def alpha_sum():
+                nc.vector.tensor_scalar(out=held["S"][:], in0=held["S"][:], scalar1=float(C), scalar2=None, op0=ALU.add)
+
+            def reciprocal():
+                held["rS"] = fin.tile([P, GROUP], F32, name="rs_g", tag="rS")
+                nc.vector.reciprocal(out=held["rS"][:], in_=held["S"][:])
+                held["pr"] = outp.tile([P, GROUP, C], F32, name="pr_g", tag="pr")
+                held["even"] = sortp.tile([P, C * GROUP], F32, name="even_g", tag="even", bufs=1)
+                held["odd"] = sortp.tile([P, C * GROUP], F32, name="odd_g", tag="odd", bufs=1)
+
+            def vacuity_of_group():
+                nc.vector.tensor_scalar(out=vacuity[:, tiles], in0=held["rS"][:], scalar1=float(C), scalar2=None, op0=ALU.mult)
+
+            def prob(s):
+                def unit():
+                    nc.vector.tensor_scalar(out=held["pr"][:, s, :], in0=held["al"][:, s, :], scalar1=held["rS"][:, s : s + 1], scalar2=None, op0=ALU.mult)
+                    if s == GROUP - 1:
+                        nc.sync.dma_start(out=prob_hbm[:, tiles, :], in_=held["pr"][:])
+
+                return unit
+
+            def sort_stage(n, d, mirrored):
+                def unit():
+                    dst = held["even"] if n % 2 == 0 else held["odd"]
+                    src = held["odd"] if n % 2 == 0 else held["even"]
+                    if n == 0:
+                        sv = held["ev"][:].rearrange("p i (n two) -> p n two i", two=2)
+                        dv = dst[:].rearrange("p (n two i) -> p n two i", two=2, i=GROUP)
+                        first, second = sv[:, :, 0, :], sv[:, :, 1, :]
+                        larger, smaller = dv[:, :, 0, :], dv[:, :, 1, :]
+                    elif mirrored:
+                        sv = src[:].rearrange("p (n two d i) -> p n two d i", two=2, d=d, i=GROUP)
+                        dv = dst[:].rearrange("p (n two d i) -> p n two d i", two=2, d=d, i=GROUP)
+                        first, second = sv[:, :, 0, :, :], sv[:, :, 1, ::-1, :]
+                        larger, smaller = dv[:, :, 0, :, :], dv[:, :, 1, :, :]
+                    else:
+                        sv = src[:].rearrange("p (n two m) -> p n two m", two=2, m=d * GROUP)
+                        dv = dst[:].rearrange("p (n two m) -> p n two m", two=2, m=d * GROUP)
+                        first, second = sv[:, :, 0, :], sv[:, :, 1, :]
+                        larger, smaller = dv[:, :, 0, :], dv[:, :, 1, :]
+                    runs = first.shape[1]
+                    parts = 2 if (g == 0 and runs > 1) else 1
+                    for part in range(parts):
+                        sel = slice(part * runs // parts, (part + 1) * runs // parts)
+                        nc.vector.tensor_tensor(out=larger[:, sel], in0=first[:, sel], in1=second[:, sel], op=ALU.max)
+                        nc.vector.tensor_tensor(out=smaller[:, sel], in0=first[:, sel], in1=second[:, sel], op=ALU.min)
+
+                return unit
+
+            def belief(s):
+                def unit():
+                    if s == 0:
+                        x_of[g] = sortp.tile([P, GROUP * C], F32, name="x_g", tag="x")
+                    nc.vector.tensor_scalar(out=x_of[g][:, s * C : (s + 1) * C], in0=held["odd"][:].rearrange("p (e i) -> p e i", i=GROUP)[:, :, s], scalar1=held["rS"][:, s : s + 1], scalar2=None, op0=ALU.mult)
+
+                return unit
+
+            def part_sums():
+                x3 = x_of[g][:].rearrange("p (t c) -> p t c", c=C)
+                nc.vector.tensor_reduce(out=sum_low[:, tiles], in_=x3[:, :, 0:ROW_SPLIT], axis=AX.X, op=ALU.add)
+                nc.vector.tensor_reduce(out=sum_high[:, tiles], in_=x3[:, :, ROW_SPLIT:C], axis=AX.X, op=ALU.add)
+
+            units = [evidence, alpha, evidence_sum, alpha_sum, reciprocal, vacuity_of_group]
+            units.extend([prob(s) for s in range(GROUP)])
+            n = 0
+            for level in range(1, LEVELS + 1):
+                for step in range(level):
+                    d = (1 << level) >> (step + 1)
+                    units.append(sort_stage(n, d, step == 0 and d > 1))
+                    n += 1
+            units.extend([belief(s) for s in range(GROUP)])
+            units.append(part_sums)
+            return units
+
+        def exp_pass(g):
+            nc.scalar.activation(out=flat(soft_of[g][:]), in_=flat(soft_of[g][:]), func=ACT.Exp)
+
+        def softplus_ln_pass(g):
+            nc.scalar.activation(out=flat(soft_of[g][:]), in_=flat(soft_of[g][:]), func=ACT.Ln, bias=one_col[:])
+
+        def belief_ln_pass(g):
+            hneg_of[g] = grp.tile([P, GROUP, C], F32, name="hneg_g", tag="hneg")
+            nc.scalar.activation(out=flat(hneg_of[g][:]), in_=x_of[g][:], func=ACT.Ln, bias=half_eps_col[:])
+
+        def halve(g):
+            nc.vector.tensor_scalar(out=flat(hneg_of[g][:]), in0=flat(hneg_of[g][:]), scalar1=-0.5, scalar2=None, op0=ALU.mult)
+
+        w_turned_of = {}
+        w_of = {}
+
+        def turn_back(g, s):
+            def unit():
+                w_sb = fin.tile([P, P], F32, name="w_sb", tag="w_sb")
+                nc.vector.tensor_copy(out=w_sb[:], in_=w_turned_of[(g, s)][:])
+                if s == 0:
+                    w_of[g] = psum_wb.tile([P, GROUP, C], F32, name="w_g", tag="w")
+                nc.tensor.transpose(w_of[g][:, s, :], w_sb[:], ident[:])
+
+            return unit
+
+        def weigh(g):
+            held = {}
+
+            def times_w():
+                held["u"] = fin.tile([P, GROUP * C], F32, name="u_g", tag="u")
+                nc.vector.scalar_tensor_tensor(out=held["u"][:], in0=x_of[g][:], scalar=EPS, in1=flat(w_of[g][:]), op0=ALU.add, op1=ALU.mult)
+
+            def minus_eps_a():
+                nc.vector.tensor_tensor(out=held["u"][:], in0=held["u"][:], in1=flat(eps_a[:]), op=ALU.subtract)
+
+            def times_x():
+                nc.vector.tensor_tensor(out=held["u"][:], in0=held["u"][:], in1=x_of[g][:], op=ALU.mult)
+
+            def sum_up():
+                nc.vector.tensor_reduce(out=weighted[:, GROUP * g : GROUP * (g + 1)], in_=held["u"][:].rearrange("p (t c) -> p t c", c=C), axis=AX.X, op=ALU.add)
+
+            return [times_w, minus_eps_a, times_x, sum_up]
+
+        def sum_rows(parity, a):
+            def unit():
+                nc.vector.tensor_reduce(out=row_sums[parity][:, a : a + SUM_ROWS], in_=th_low[parity][:, a : a + SUM_ROWS, 0 : a + SUM_ROWS - 1], axis=AX.X, op=ALU.add)
+
+            return unit
+
+        def rows_of_group(g, chain, feed, carried):
+            total = GROUP * PAIRS
+            marked = []
+            for pos in range(len(chain)):
+                marked.append(((pos + 1) * CHAIN_SPAN * total / len(chain), chain[pos]))
+            for pos in range(len(feed)):
+                marked.append(((pos + 1) * FEED_SPAN * total / len(feed), feed[pos]))
+            for pos in range(len(carried)):
+                marked.append((AFTER_TILE + pos * AFTER_STEP, carried[pos]))
+            blocks = ROW_SPLIT // SUM_ROWS
+            for s in range(GROUP):
+                for b in range(blocks):
+                    written = (b + 1) * SUM_ROWS * ((b + 1) * SUM_ROWS - 1) // 2
+                    marked.append((s * PAIRS + max(written, (b + 1) * SUM_SPAN * PAIRS / blocks), sum_rows((GROUP * g + s) % 2, b * SUM_ROWS)))
+                if s < GROUP - 1:
+                    marked.append(((s + 1) * PAIRS + AFTER_TILE, turn_back(g, s)))
+            marked = sorted(marked, key=lambda pair: pair[0])
+
+            hneg = hneg_of[g]
+            elements = 0
+            due = 0
+            for s in range(GROUP):
+                parity = (GROUP * g + s) % 2
+                w_turned = psum_w.tile([P, P], F32, name="w_turned", tag="w_turned")
+                w_turned_of[(g, s)] = w_turned
+                nc.tensor.matmul(out=w_turned[:], lhsT=a_row[:], rhs=ident[:], is_transpose=True, start=True, stop=False)
+                for j in range(1, C):
+                    row = th_low[parity][:, j, :] if j < ROW_SPLIT else th_high[:, j - ROW_SPLIT, :]
+                    nc.scalar.activation(out=row[:, 0:j], in_=hneg[:, s, 0:j], func=ACT.Tanh, bias=hneg[:, s, j : j + 1], scale=-1.0)
+                    if j >= ROW_SPLIT:
+                        nc.tensor.matmul(out=w_turned[:], lhsT=row, rhs=ident[:], is_transpose=True, start=False, stop=False)
+                    elements += j
+                    while due < len(marked) and marked[due][0] <= elements:
+                        marked[due][1]()
+                        due += 1
+                nc.tensor.matmul(out=w_turned[:], lhsT=row_sums[parity][:], rhs=ident[:], is_transpose=True, start=False, stop=True)
+            assert due == len(marked)
+            return [turn_back(g, GROUP - 1)] + weigh(g)
+
+        for unit in stage_a(0):
+            unit()
+        exp_pass(0)
+        softplus_ln_pass(0)
+        ahead = stage_a(1)
+        for unit in ahead[:3]:
+            unit()
+        for unit in interleave(stage_b(0), ahead[3:]):
+            unit()
+        exp_pass(1)
+        belief_ln_pass(0)
+        softplus_ln_pass(1)
+        halve(0)
+        carried = []
+        for g in range(GROUPS):
+            chain = stage_b(g + 1) if g + 1 < GROUPS else []
+            feed = stage_a(g + 2) if g + 2 < GROUPS else []
+            carried = rows_of_group(g, chain, feed, carried)
+            if g + 2 < GROUPS:
+                exp_pass(g + 2)
+            if g + 1 < GROUPS:
+                belief_ln_pass(g + 1)
+            if g + 2 < GROUPS:
+                softplus_ln_pass(g + 2)
+            if g + 1 < GROUPS:
+                halve(g + 1)
+
+        cross = const.tile([P, TILES], F32, name="cross")
+        nc.vector.scalar_tensor_tensor(out=cross[:], in0=sum_low[:], scalar=2.0, in1=sum_high[:], op0=ALU.mult, op1=ALU.add)
+        nc.vector.tensor_tensor(out=cross[:], in0=cross[:], in1=sum_high[:], op=ALU.mult)
+        for unit in carried:
+            unit()
+        nc.vector.tensor_tensor(out=dissonance[:], in0=cross[:], in1=weighted[:], op=ALU.add)
+        nc.sync.dma_start(out=vacuity_hbm, in_=vacuity[:])
+        nc.sync.dma_start(out=dissonance_hbm, in_=dissonance[:])

@@ -19,35 +19,41 @@ AX = mybir.AxisListType
 
 P = 128
 TILES = ROWS // P
-GROUP = 4
+QUAD = 4
+GROUP = 8
 GROUPS = TILES // GROUP
+QUADS = GROUP // QUAD
 PASSES = K // (4 * P)
 WORDS = 2 * P
 FIRST_LOAD = 2
 LEVELS = 7
+STAGES = LEVELS * (LEVELS + 1) // 2
 EPS = 1e-8
-PAIRS = C * (C - 1) // 2
+CONSTANT = 1.99999999975556
+EXPONENTS = (1.00000003251, 2.00018891269, 2.98310507162, 4.43669433027, 4.72915341974, 5.05369642201, 5.80774242344, 7.13256179473, 8.43355250839)
+WEIGHTS = (-1.99999945329247, 2.00220339501363, -1.89071956839634, 10.7493049500827, -18.1703486275972, 9.20543703239164, -0.941251246893103, 0.0485658928379882, -0.00319237421115004)
+MODES = len(EXPONENTS)
+RESET = -10000.0
 
-ROW_SPLIT = 72
-SUM_ROWS = 8
 
-CHAIN_SPAN = 0.95
-FEED_SPAN = 0.9
-SUM_SPAN = 0.9
-AFTER_TILE = 2500
-AFTER_STEP = 800
+def fit_error(r):
+    return abs(CONSTANT + sum(WEIGHTS[m] * r ** EXPONENTS[m] for m in range(MODES)) - 2.0 / (1.0 + r))
+
+
+assert max(fit_error(i / 4096.0) for i in range(4097)) < 4e-10
+assert max(fit_error(0.5 ** i) for i in range(12, 80)) < 4e-10
 
 
 def flat(ap):
     return ap.rearrange("p t c -> p (t c)")
 
 
-def interleave(a, b):
-    out = []
-    for i in range(max(len(a), len(b))):
-        out.extend(a[i : i + 1])
-        out.extend(b[i : i + 1])
-    return out
+LEAD = 3
+LATE_SCANS = 2
+FEED_FROM, FEED_TO = 0.03, 0.86
+POWERS_TO = 0.30
+SCANS_FROM, SCANS_TO = 0.34, 0.89
+AFTER_SCAN = 0.05
 
 
 def tile_evidentialhead_pb_kernel(tc, h_act_bytes, h_act_scale, W3, b3, out_0, out_1, out_2, out_3, out_4):
@@ -59,6 +65,7 @@ def tile_evidentialhead_pb_kernel(tc, h_act_bytes, h_act_scale, W3, b3, out_0, o
         grp = ctx.enter_context(tc.tile_pool(name="grp", bufs=2))
         outp = ctx.enter_context(tc.tile_pool(name="outp", bufs=1))
         sortp = ctx.enter_context(tc.tile_pool(name="sortp", bufs=3))
+        modes = ctx.enter_context(tc.tile_pool(name="modes", bufs=2))
         fin = ctx.enter_context(tc.tile_pool(name="fin", bufs=2))
         psum_t = ctx.enter_context(tc.psum_pool(name="psum_t", bufs=2))
         psum_acc = ctx.enter_context(tc.psum_pool(name="psum_acc", bufs=2))
@@ -80,341 +87,330 @@ def tile_evidentialhead_pb_kernel(tc, h_act_bytes, h_act_scale, W3, b3, out_0, o
         nc.sync.dma_start(out=hbytes[:, 0:FIRST_LOAD, :], in_=bytes_hbm[:, 0:FIRST_LOAD, :])
         nc.sync.dma_start(out=w_raw[:], in_=W3.rearrange("(q p j) n -> p q j n", p=P, j=4))
         nc.sync.dma_start(out=bias_bc[:], in_=b3.partition_broadcast(P))
-        for t in range(FIRST_LOAD, TILES, GROUP):
-            e = min(t + GROUP, TILES)
+        for t in range(FIRST_LOAD, TILES, QUAD):
+            e = min(t + QUAD, TILES)
             nc.sync.dma_start(out=hbytes[:, t:e, :], in_=bytes_hbm[:, t:e, :])
 
-        zeros = const.tile([P, SUM_ROWS, P], F32, name="zeros")
+        zeros = const.tile([P, C], F32, name="zeros")
         nc.gpsimd.memset(zeros[:], 0.0)
         ident = const.tile([P, P], F32, name="ident")
         make_identity(nc, ident[:])
         index_i = const.tile([P, C], I32, name="index_i")
         nc.gpsimd.iota(out=index_i[:], pattern=[[1, C]], base=0, channel_multiplier=0)
+        lam = [const.tile([P, GROUP, C], F32, name="lam0"), const.tile([P, GROUP, C], F32, name="lam1")]
+        for lam_tile in lam:
+            nc.gpsimd.memset(lam_tile[:], RESET)
 
         warm = const.tile([P, 1], F32, name="warm")
-        nc.scalar.activation(out=warm[:], in_=zeros[:, 0, 0:1], func=ACT.Exp)
-
-        th_high = const.tile([P, P - ROW_SPLIT, P], F32, name="th_high")
-        th_low = [const.tile([P, ROW_SPLIT, ROW_SPLIT], F32, name="th_low0"), const.tile([P, ROW_SPLIT, ROW_SPLIT], F32, name="th_low1")]
-        row_sums = [const.tile([P, P], F32, name="row_sums0"), const.tile([P, P], F32, name="row_sums1")]
-        for a in range(0, ROW_SPLIT, SUM_ROWS):
-            for low in th_low:
-                nc.scalar.copy(out=low[:, a : a + SUM_ROWS, a:ROW_SPLIT], in_=zeros[:, :, a:ROW_SPLIT])
-        for sums_tile in row_sums:
-            nc.scalar.copy(out=sums_tile[:, ROW_SPLIT:P], in_=zeros[:, 0, ROW_SPLIT:P])
-        for a in range(ROW_SPLIT, P, SUM_ROWS):
-            nc.scalar.copy(out=th_high[:, a - ROW_SPLIT : a - ROW_SPLIT + SUM_ROWS, a:P], in_=zeros[:, :, a:P])
-
-        a_row = const.tile([P, C], F32, name="a_row")
-        nc.vector.tensor_copy(out=a_row[:], in_=index_i[:])
-        nc.vector.tensor_scalar(out=a_row[:, 0:ROW_SPLIT], in0=a_row[:, 0:ROW_SPLIT], scalar1=float(ROW_SPLIT - P), scalar2=None, op0=ALU.add)
-        nc.vector.tensor_scalar(out=a_row[:, ROW_SPLIT:P], in0=a_row[:, ROW_SPLIT:P], scalar1=float(-P), scalar2=None, op0=ALU.add)
-        eps_a = const.tile([P, GROUP, C], F32, name="eps_a")
-        for s in range(GROUP):
-            nc.vector.tensor_scalar(out=eps_a[:, s, :], in0=a_row[:], scalar1=EPS, scalar2=None, op0=ALU.mult)
-        one_col = const.tile([P, 1], F32, name="one_col")
-        nc.vector.memset(one_col[:], 1.0)
-        half_eps_col = const.tile([P, 1], F32, name="half_eps_col")
-        nc.vector.tensor_scalar(out=half_eps_col[:], in0=zeros[:, 0, 0:1], scalar1=0.5 * EPS, scalar2=None, op0=ALU.add)
+        nc.scalar.activation(out=warm[:], in_=zeros[:, 0:1], func=ACT.Exp)
 
         w_grouped = const.tile([P, PASSES, C, 4], BF16, name="w_grouped", align_bytes=64)
         nc.vector.tensor_copy(out=w_grouped[:], in_=w_raw[:].rearrange("p q j n -> p q n j"))
         w_codes = const.tile([P, PASSES * C], U32, name="w_codes", align_bytes=64)
         w_scales = const.tile([P, PASSES * C], U8, name="w_scales", align_bytes=64)
-        bias_grp = const.tile([P, GROUP, C], BF16, name="bias_grp")
-        for s in range(GROUP):
-            nc.vector.tensor_copy(out=bias_grp[:, s, :], in_=bias_bc[:])
+        bias_quad = const.tile([P, QUAD, C], BF16, name="bias_quad")
+        for s in range(QUAD):
+            nc.vector.tensor_copy(out=bias_quad[:, s, :], in_=bias_bc[:])
         nc.vector.quantize_mx(out=w_codes[:].bitcast(FP8X4), scales=w_scales[:], in_=w_grouped[:].rearrange("p q n j -> p (q n j)"))
+
+        one_col = const.tile([P, 1], F32, name="one_col")
+        nc.vector.memset(one_col[:], 1.0)
+        half_eps_col = const.tile([P, 1], F32, name="half_eps_col")
+        nc.vector.tensor_scalar(out=half_eps_col[:], in0=zeros[:, 0:1], scalar1=0.5 * EPS, scalar2=None, op0=ALU.add)
+
+        j_row = const.tile([P, C], F32, name="j_row")
+        a_row = const.tile([P, C], F32, name="a_row")
+        eps_j = const.tile([P, QUAD, C], F32, name="eps_j")
+        c_rows = const.tile([P, MODES, C], F32, name="c_rows")
+
+        def constants():
+            nc.vector.tensor_copy(out=j_row[:], in_=index_i[:])
+            nc.vector.tensor_scalar(out=a_row[:], in0=j_row[:], scalar1=CONSTANT, scalar2=-sum(WEIGHTS), op0=ALU.mult, op1=ALU.add)
+            for s in range(QUAD):
+                nc.vector.tensor_scalar(out=eps_j[:, s, :], in0=j_row[:], scalar1=EPS, scalar2=None, op0=ALU.mult)
+            for m in range(MODES):
+                nc.vector.tensor_scalar(out=c_rows[:, m, :], in0=zeros[:], scalar1=WEIGHTS[m], scalar2=None, op0=ALU.add)
 
         vacuity = const.tile([P, TILES], F32, name="vacuity")
         dissonance = const.tile([P, TILES], F32, name="dissonance")
-        weighted = const.tile([P, TILES], F32, name="weighted")
-        sum_low = const.tile([P, TILES], F32, name="sum_low")
-        sum_high = const.tile([P, TILES], F32, name="sum_high")
 
         logit_of = [None] * GROUPS
         soft_of = [None] * GROUPS
+        sorted_of = [None] * GROUPS
+        rs_of = [None] * GROUPS
         x_of = [None] * GROUPS
-        hneg_of = [None] * GROUPS
+        e_of = {}
 
-        def stage_a(g):
-            turned_of, grouped_of, held = {}, {}, {}
+        def feed(g):
+            turned_of, grouped_of, acc_of = {}, {}, {}
 
             def widen(s):
-                def unit():
-                    if s == 0:
-                        logit_of[g] = grp.tile([P, GROUP, C], F32, name="logit_g", tag="logit")
-                        soft_of[g] = grp.tile([P, GROUP, C], F32, name="soft_g", tag="soft")
-                    h_bf = stage.tile([P, K], BF16, name="h_bf", tag="h_bf", align_bytes=64)
-                    nc.vector.tensor_tensor(out=h_bf[:], in0=hbytes[:, GROUP * g + s, :].bitcast(FP8), in1=scale_bc[:], op=ALU.mult)
-                    words = h_bf[:].bitcast(F32)
-                    turned = psum_t.tile([P, PASSES, 2, P], F32, name="turned", tag="turned")
-                    for q in range(PASSES):
-                        for u in range(2):
-                            nc.tensor.transpose(turned[:, q, u, :], words[:, WORDS * q + u : WORDS * (q + 1) : 2], ident[:])
-                    turned_of[s] = turned
-
-                return unit
+                if s == 0:
+                    logit_of[g] = grp.tile([P, GROUP, C], F32, name="logit_g", tag="logit")
+                    soft_of[g] = grp.tile([P, GROUP, C], F32, name="soft_g", tag="soft")
+                h_bf = stage.tile([P, K], BF16, name="h_bf", tag="h_bf", align_bytes=64)
+                nc.vector.tensor_tensor(out=h_bf[:], in0=hbytes[:, GROUP * g + s, :].bitcast(FP8), in1=scale_bc[:], op=ALU.mult)
+                words = h_bf[:].bitcast(F32)
+                turned = psum_t.tile([P, PASSES, 2, P], F32, name="turned", tag="turned")
+                for q in range(PASSES):
+                    for u in range(2):
+                        nc.tensor.transpose(turned[:, q, u, :], words[:, WORDS * q + u : WORDS * (q + 1) : 2], ident[:])
+                turned_of[s] = turned
 
             def copy_out(s):
-                def unit():
-                    grouped = stage.tile([P, PASSES, P, 4], BF16, name="grouped", tag="grouped", align_bytes=64)
-                    nc.vector.tensor_copy(out=grouped[:].bitcast(F32), in_=turned_of[s][:].rearrange("p q u r -> p q r u"))
-                    grouped_of[s] = grouped
-
-                return unit
+                grouped = stage.tile([P, PASSES, P, 4], BF16, name="grouped", tag="grouped", align_bytes=64)
+                nc.scalar.copy(out=grouped[:].bitcast(F32), in_=turned_of[s][:].rearrange("p q u r -> p q r u"))
+                grouped_of[s] = grouped
 
             def quantise(s):
+                codes = stage.tile([P, PASSES * P], U32, name="codes", tag="codes", align_bytes=64)
+                scales = stage.tile([P, PASSES * P], U8, name="scales", tag="scales", align_bytes=64)
+                nc.vector.quantize_mx(out=codes[:].bitcast(FP8X4), scales=scales[:], in_=grouped_of[s][:].rearrange("p q r t -> p (q r t)"))
+                if s % QUAD == 0:
+                    acc_of[s // QUAD] = psum_acc.tile([P, QUAD, C], F32, name="acc", tag="acc")
+                for q in range(PASSES):
+                    cols = slice(P * q, P * (q + 1))
+                    nc.tensor.matmul_mx(
+                        out=acc_of[s // QUAD][:, s % QUAD, :],
+                        lhsT=codes[:, cols].bitcast(FP8X4),
+                        lhsT_scale=scales[:, cols],
+                        rhs=w_codes[:, cols].bitcast(FP8X4),
+                        rhs_scale=w_scales[:, cols],
+                        start=(q == 0),
+                        stop=(q == PASSES - 1),
+                    )
+
+            def add_bias(h):
+                nc.vector.tensor_tensor(out=logit_of[g][:, QUAD * h : QUAD * (h + 1), :], in0=acc_of[h][:], in1=bias_quad[:], op=ALU.add)
+
+            def abs_exp(h):
+                tiles = slice(QUAD * h, QUAD * (h + 1))
+                nc.scalar.activation(out=soft_of[g][:, tiles, :], in_=logit_of[g][:, tiles, :], func=ACT.Abs)
+                nc.scalar.activation(out=soft_of[g][:, tiles, :], in_=soft_of[g][:, tiles, :], func=ACT.Exp, scale=-1.0)
+
+            def step(i):
                 def unit():
-                    codes = stage.tile([P, PASSES * P], U32, name="codes", tag="codes", align_bytes=64)
-                    scales = stage.tile([P, PASSES * P], U8, name="scales", tag="scales", align_bytes=64)
-                    nc.vector.quantize_mx(out=codes[:].bitcast(FP8X4), scales=scales[:], in_=grouped_of[s][:].rearrange("p q r t -> p (q r t)"))
-                    if s == 0:
-                        held["acc"] = psum_acc.tile([P, GROUP, C], F32, name="acc", tag="acc")
-                    for q in range(PASSES):
-                        cols = slice(P * q, P * (q + 1))
-                        nc.tensor.matmul_mx(
-                            out=held["acc"][:, s, :],
-                            lhsT=codes[:, cols].bitcast(FP8X4),
-                            lhsT_scale=scales[:, cols],
-                            rhs=w_codes[:, cols].bitcast(FP8X4),
-                            rhs_scale=w_scales[:, cols],
-                            start=(q == 0),
-                            stop=(q == PASSES - 1),
-                        )
+                    if i < GROUP:
+                        widen(i)
+                    if 1 <= i <= GROUP:
+                        copy_out(i - 1)
+                    if 2 <= i <= GROUP + 1:
+                        quantise(i - 2)
+                    if i >= 3 and (i - 3) % QUAD == QUAD - 1:
+                        add_bias((i - 3) // QUAD)
+                    if i >= 4 and (i - 4) % QUAD == QUAD - 1:
+                        abs_exp((i - 4) // QUAD)
 
                 return unit
 
-            def add_bias():
-                nc.vector.tensor_tensor(out=logit_of[g][:], in0=held["acc"][:], in1=bias_grp[:], op=ALU.add)
+            return [step(i) for i in range(GROUP + 4)]
 
-            def neg_abs():
-                v = flat(logit_of[g][:])
-                nc.vector.scalar_tensor_tensor(out=flat(soft_of[g][:]), in0=v, scalar=-1.0, in1=v, op0=ALU.mult, op1=ALU.min)
+        held = [dict() for g in range(GROUPS)]
 
-            units = []
-            for s in range(GROUP + 2):
-                if s < GROUP:
-                    units.append(widen(s))
-                if 1 <= s <= GROUP:
-                    units.append(copy_out(s - 1))
-                if s >= 2:
-                    units.append(quantise(s - 2))
-            return units + [add_bias, neg_abs]
+        def ln_softplus(g):
+            nc.scalar.activation(out=flat(soft_of[g][:]), in_=flat(soft_of[g][:]), func=ACT.Ln, bias=one_col[:])
 
-        def stage_b(g):
+        def evidence(g):
             tiles = slice(GROUP * g, GROUP * (g + 1))
-            held = {}
+            held[g]["ev"] = outp.tile([P, GROUP, C], F32, name="ev_g", tag="ev")
+            nc.vector.scalar_tensor_tensor(out=flat(held[g]["ev"][:]), in0=flat(logit_of[g][:]), scalar=0.0, in1=flat(soft_of[g][:]), op0=ALU.max, op1=ALU.add)
+            nc.sync.dma_start(out=evidence_hbm[:, tiles, :], in_=held[g]["ev"][:])
 
-            def evidence():
-                held["ev"] = outp.tile([P, GROUP, C], F32, name="ev_g", tag="ev")
-                nc.vector.scalar_tensor_tensor(out=flat(held["ev"][:]), in0=flat(logit_of[g][:]), scalar=0.0, in1=flat(soft_of[g][:]), op0=ALU.max, op1=ALU.add)
-                nc.sync.dma_start(out=evidence_hbm[:, tiles, :], in_=held["ev"][:])
+        def alpha(g, s):
+            def unit():
+                if s == 0:
+                    held[g]["al"] = outp.tile([P, GROUP, C], F32, name="al_g", tag="al")
+                    held[g]["S"] = fin.tile([P, GROUP], F32, name="s_g", tag="S")
+                nc.scalar.activation(out=held[g]["al"][:, s, :], in_=held[g]["ev"][:, s, :], func=ACT.Identity, bias=one_col[:], accum_out=held[g]["S"][:, s : s + 1])
+                if s == GROUP - 1:
+                    nc.sync.dma_start(out=alpha_hbm[:, GROUP * g : GROUP * (g + 1), :], in_=held[g]["al"][:])
 
-            def alpha():
-                held["al"] = outp.tile([P, GROUP, C], F32, name="al_g", tag="al")
-                nc.vector.tensor_scalar(out=flat(held["al"][:]), in0=flat(held["ev"][:]), scalar1=1.0, scalar2=None, op0=ALU.add)
-                nc.sync.dma_start(out=alpha_hbm[:, tiles, :], in_=held["al"][:])
+            return unit
 
-            def evidence_sum():
-                held["S"] = fin.tile([P, GROUP], F32, name="s_g", tag="S")
-                nc.vector.tensor_reduce(out=held["S"][:], in_=held["ev"][:], axis=AX.X, op=ALU.add)
+        def reciprocal(g):
+            def unit():
+                rs_of[g] = fin.tile([P, GROUP], F32, name="rs_g", tag="rS")
+                nc.vector.reciprocal(out=rs_of[g][:], in_=held[g]["S"][:])
+                nc.vector.tensor_scalar(out=vacuity[:, GROUP * g : GROUP * (g + 1)], in0=rs_of[g][:], scalar1=float(C), scalar2=None, op0=ALU.mult)
 
-            def alpha_sum():
-                nc.vector.tensor_scalar(out=held["S"][:], in0=held["S"][:], scalar1=float(C), scalar2=None, op0=ALU.add)
+            return unit
 
-            def reciprocal():
-                held["rS"] = fin.tile([P, GROUP], F32, name="rs_g", tag="rS")
-                nc.vector.reciprocal(out=held["rS"][:], in_=held["S"][:])
-                held["pr"] = outp.tile([P, GROUP, C], F32, name="pr_g", tag="pr")
-                held["even"] = sortp.tile([P, C * GROUP], F32, name="even_g", tag="even", bufs=1)
-                held["odd"] = sortp.tile([P, C * GROUP], F32, name="odd_g", tag="odd", bufs=1)
+        def prob(g, s):
+            def unit():
+                if s == 0:
+                    held[g]["pr"] = outp.tile([P, GROUP, C], F32, name="pr_g", tag="pr")
+                nc.scalar.activation(out=held[g]["pr"][:, s, :], in_=held[g]["al"][:, s, :], func=ACT.Copy, scale=rs_of[g][:, s : s + 1])
+                if s == GROUP - 1:
+                    nc.sync.dma_start(out=prob_hbm[:, GROUP * g : GROUP * (g + 1), :], in_=held[g]["pr"][:])
 
-            def vacuity_of_group():
-                nc.vector.tensor_scalar(out=vacuity[:, tiles], in0=held["rS"][:], scalar1=float(C), scalar2=None, op0=ALU.mult)
+            return unit
 
-            def prob(s):
-                def unit():
-                    nc.vector.tensor_scalar(out=held["pr"][:, s, :], in0=held["al"][:, s, :], scalar1=held["rS"][:, s : s + 1], scalar2=None, op0=ALU.mult)
-                    if s == GROUP - 1:
-                        nc.sync.dma_start(out=prob_hbm[:, tiles, :], in_=held["pr"][:])
+        def sort_stage(g, n, d, mirrored, parts):
+            def unit():
+                if n == 0:
+                    held[g]["even"] = sortp.tile([P, C * GROUP], F32, name="even_g", tag="even", bufs=1)
+                    held[g]["odd"] = sortp.tile([P, C * GROUP], F32, name="odd_g", tag="odd", bufs=1)
+                dst = held[g]["even"] if n % 2 == 0 else held[g]["odd"]
+                src = held[g]["odd"] if n % 2 == 0 else held[g]["even"]
+                if n == 0:
+                    sv = held[g]["ev"][:].rearrange("p i (n two) -> p n two i", two=2)
+                    dv = dst[:].rearrange("p (n two i) -> p n two i", two=2, i=GROUP)
+                    first, second = sv[:, :, 0, :], sv[:, :, 1, :]
+                    larger, smaller = dv[:, :, 0, :], dv[:, :, 1, :]
+                elif mirrored:
+                    sv = src[:].rearrange("p (n two d i) -> p n two d i", two=2, d=d, i=GROUP)
+                    dv = dst[:].rearrange("p (n two d i) -> p n two d i", two=2, d=d, i=GROUP)
+                    first, second = sv[:, :, 0, :, :], sv[:, :, 1, ::-1, :]
+                    larger, smaller = dv[:, :, 0, :, :], dv[:, :, 1, :, :]
+                else:
+                    sv = src[:].rearrange("p (n two m) -> p n two m", two=2, m=d * GROUP)
+                    dv = dst[:].rearrange("p (n two m) -> p n two m", two=2, m=d * GROUP)
+                    first, second = sv[:, :, 0, :], sv[:, :, 1, :]
+                    larger, smaller = dv[:, :, 0, :], dv[:, :, 1, :]
+                runs = first.shape[1]
+                cut = parts if runs > 1 else 1
+                for part in range(cut):
+                    sel = slice(part * runs // cut, (part + 1) * runs // cut)
+                    nc.vector.tensor_tensor(out=larger[:, sel], in0=first[:, sel], in1=second[:, sel], op=ALU.max)
+                    nc.vector.tensor_tensor(out=smaller[:, sel], in0=first[:, sel], in1=second[:, sel], op=ALU.min)
 
-                return unit
+            return unit
 
-            def sort_stage(n, d, mirrored):
-                def unit():
-                    dst = held["even"] if n % 2 == 0 else held["odd"]
-                    src = held["odd"] if n % 2 == 0 else held["even"]
-                    if n == 0:
-                        sv = held["ev"][:].rearrange("p i (n two) -> p n two i", two=2)
-                        dv = dst[:].rearrange("p (n two i) -> p n two i", two=2, i=GROUP)
-                        first, second = sv[:, :, 0, :], sv[:, :, 1, :]
-                        larger, smaller = dv[:, :, 0, :], dv[:, :, 1, :]
-                    elif mirrored:
-                        sv = src[:].rearrange("p (n two d i) -> p n two d i", two=2, d=d, i=GROUP)
-                        dv = dst[:].rearrange("p (n two d i) -> p n two d i", two=2, d=d, i=GROUP)
-                        first, second = sv[:, :, 0, :, :], sv[:, :, 1, ::-1, :]
-                        larger, smaller = dv[:, :, 0, :, :], dv[:, :, 1, :, :]
-                    else:
-                        sv = src[:].rearrange("p (n two m) -> p n two m", two=2, m=d * GROUP)
-                        dv = dst[:].rearrange("p (n two m) -> p n two m", two=2, m=d * GROUP)
-                        first, second = sv[:, :, 0, :], sv[:, :, 1, :]
-                        larger, smaller = dv[:, :, 0, :], dv[:, :, 1, :]
-                    runs = first.shape[1]
-                    parts = 2 if (g == 0 and runs > 1) else 1
-                    for part in range(parts):
-                        sel = slice(part * runs // parts, (part + 1) * runs // parts)
-                        nc.vector.tensor_tensor(out=larger[:, sel], in0=first[:, sel], in1=second[:, sel], op=ALU.max)
-                        nc.vector.tensor_tensor(out=smaller[:, sel], in0=first[:, sel], in1=second[:, sel], op=ALU.min)
-
-                return unit
-
-            def belief(s):
-                def unit():
-                    if s == 0:
-                        x_of[g] = sortp.tile([P, GROUP * C], F32, name="x_g", tag="x")
-                    nc.vector.tensor_scalar(out=x_of[g][:, s * C : (s + 1) * C], in0=held["odd"][:].rearrange("p (e i) -> p e i", i=GROUP)[:, :, s], scalar1=held["rS"][:, s : s + 1], scalar2=None, op0=ALU.mult)
-
-                return unit
-
-            def part_sums():
-                x3 = x_of[g][:].rearrange("p (t c) -> p t c", c=C)
-                nc.vector.tensor_reduce(out=sum_low[:, tiles], in_=x3[:, :, 0:ROW_SPLIT], axis=AX.X, op=ALU.add)
-                nc.vector.tensor_reduce(out=sum_high[:, tiles], in_=x3[:, :, ROW_SPLIT:C], axis=AX.X, op=ALU.add)
-
-            units = [evidence, alpha, evidence_sum, alpha_sum, reciprocal, vacuity_of_group]
-            units.extend([prob(s) for s in range(GROUP)])
-            n = 0
+        def sort_chain(g, parts):
+            units = []
             for level in range(1, LEVELS + 1):
                 for step in range(level):
                     d = (1 << level) >> (step + 1)
-                    units.append(sort_stage(n, d, step == 0 and d > 1))
-                    n += 1
-            units.extend([belief(s) for s in range(GROUP)])
-            units.append(part_sums)
+                    units.append(sort_stage(g, len(units), d, step == 0 and d > 1, parts))
             return units
 
-        def exp_pass(g):
-            nc.scalar.activation(out=flat(soft_of[g][:]), in_=flat(soft_of[g][:]), func=ACT.Exp)
+        def belief(g, s):
+            if s == 0:
+                x_of[g] = sortp.tile([P, GROUP * C], F32, name="x_g", tag="x")
+            nc.scalar.activation(out=x_of[g][:, s * C : (s + 1) * C], in_=held[g]["odd"][:].rearrange("p (e i) -> p e i", i=GROUP)[:, :, s], func=ACT.Copy, scale=rs_of[g][:, s : s + 1])
 
-        def softplus_ln_pass(g):
-            nc.scalar.activation(out=flat(soft_of[g][:]), in_=flat(soft_of[g][:]), func=ACT.Ln, bias=one_col[:])
+        def ln_belief(g):
+            held[g]["L"] = grp.tile([P, GROUP, C], F32, name="l_g", tag="L")
+            nc.scalar.activation(out=flat(held[g]["L"][:]), in_=x_of[g][:], func=ACT.Ln, bias=half_eps_col[:])
 
-        def belief_ln_pass(g):
-            hneg_of[g] = grp.tile([P, GROUP, C], F32, name="hneg_g", tag="hneg")
-            nc.scalar.activation(out=flat(hneg_of[g][:]), in_=x_of[g][:], func=ACT.Ln, bias=half_eps_col[:])
+        def steps_of_l(g):
+            nc.vector.tensor_tensor(out=lam[g % 2][:, :, 1:C], in0=held[g]["L"][:, :, 1:C], in1=held[g]["L"][:, :, 0 : C - 1], op=ALU.subtract)
 
-        def halve(g):
-            nc.vector.tensor_scalar(out=flat(hneg_of[g][:]), in0=flat(hneg_of[g][:]), scalar1=-0.5, scalar2=None, op0=ALU.mult)
+        def power(g, h, m):
+            def unit():
+                if m == 0:
+                    e_of[(g, h)] = modes.tile([P, QUAD, MODES, C], F32, name="e_q", tag="e")
+                nc.scalar.activation(out=e_of[(g, h)][:, :, m, :], in_=lam[g % 2][:, QUAD * h : QUAD * (h + 1), :], func=ACT.Exp, scale=EXPONENTS[m])
+
+            return unit
 
         w_turned_of = {}
         w_of = {}
 
-        def turn_back(g, s):
+        def scan(g, s):
             def unit():
-                w_sb = fin.tile([P, P], F32, name="w_sb", tag="w_sb")
-                nc.vector.tensor_copy(out=w_sb[:], in_=w_turned_of[(g, s)][:])
-                if s == 0:
-                    w_of[g] = psum_wb.tile([P, GROUP, C], F32, name="w_g", tag="w")
-                nc.tensor.transpose(w_of[g][:, s, :], w_sb[:], ident[:])
-
-            return unit
-
-        def weigh(g):
-            held = {}
-
-            def times_w():
-                held["u"] = fin.tile([P, GROUP * C], F32, name="u_g", tag="u")
-                nc.vector.scalar_tensor_tensor(out=held["u"][:], in0=x_of[g][:], scalar=EPS, in1=flat(w_of[g][:]), op0=ALU.add, op1=ALU.mult)
-
-            def minus_eps_a():
-                nc.vector.tensor_tensor(out=held["u"][:], in0=held["u"][:], in1=flat(eps_a[:]), op=ALU.subtract)
-
-            def times_x():
-                nc.vector.tensor_tensor(out=held["u"][:], in0=held["u"][:], in1=x_of[g][:], op=ALU.mult)
-
-            def sum_up():
-                nc.vector.tensor_reduce(out=weighted[:, GROUP * g : GROUP * (g + 1)], in_=held["u"][:].rearrange("p (t c) -> p t c", c=C), axis=AX.X, op=ALU.add)
-
-            return [times_w, minus_eps_a, times_x, sum_up]
-
-        def sum_rows(parity, a):
-            def unit():
-                nc.vector.tensor_reduce(out=row_sums[parity][:, a : a + SUM_ROWS], in_=th_low[parity][:, a : a + SUM_ROWS, 0 : a + SUM_ROWS - 1], axis=AX.X, op=ALU.add)
-
-            return unit
-
-        def rows_of_group(g, chain, feed, carried):
-            total = GROUP * PAIRS
-            marked = []
-            for pos in range(len(chain)):
-                marked.append(((pos + 1) * CHAIN_SPAN * total / len(chain), chain[pos]))
-            for pos in range(len(feed)):
-                marked.append(((pos + 1) * FEED_SPAN * total / len(feed), feed[pos]))
-            for pos in range(len(carried)):
-                marked.append((AFTER_TILE + pos * AFTER_STEP, carried[pos]))
-            blocks = ROW_SPLIT // SUM_ROWS
-            for s in range(GROUP):
-                for b in range(blocks):
-                    written = (b + 1) * SUM_ROWS * ((b + 1) * SUM_ROWS - 1) // 2
-                    marked.append((s * PAIRS + max(written, (b + 1) * SUM_SPAN * PAIRS / blocks), sum_rows((GROUP * g + s) % 2, b * SUM_ROWS)))
-                if s < GROUP - 1:
-                    marked.append(((s + 1) * PAIRS + AFTER_TILE, turn_back(g, s)))
-            marked = sorted(marked, key=lambda pair: pair[0])
-
-            hneg = hneg_of[g]
-            elements = 0
-            due = 0
-            for s in range(GROUP):
-                parity = (GROUP * g + s) % 2
+                y = modes.tile([P, MODES * C], F32, name="y_t", tag="y", bufs=3)
+                nc.vector.tensor_tensor_scan(
+                    out=y[:],
+                    data0=e_of[(g, s // QUAD)][:, s % QUAD, :, :].rearrange("p k j -> p (k j)"),
+                    data1=c_rows[:].rearrange("p k j -> p (k j)"),
+                    initial=0.0,
+                    op0=ALU.mult,
+                    op1=ALU.add,
+                )
                 w_turned = psum_w.tile([P, P], F32, name="w_turned", tag="w_turned")
                 w_turned_of[(g, s)] = w_turned
                 nc.tensor.matmul(out=w_turned[:], lhsT=a_row[:], rhs=ident[:], is_transpose=True, start=True, stop=False)
-                for j in range(1, C):
-                    row = th_low[parity][:, j, :] if j < ROW_SPLIT else th_high[:, j - ROW_SPLIT, :]
-                    nc.scalar.activation(out=row[:, 0:j], in_=hneg[:, s, 0:j], func=ACT.Tanh, bias=hneg[:, s, j : j + 1], scale=-1.0)
-                    if j >= ROW_SPLIT:
-                        nc.tensor.matmul(out=w_turned[:], lhsT=row, rhs=ident[:], is_transpose=True, start=False, stop=False)
-                    elements += j
-                    while due < len(marked) and marked[due][0] <= elements:
-                        marked[due][1]()
-                        due += 1
-                nc.tensor.matmul(out=w_turned[:], lhsT=row_sums[parity][:], rhs=ident[:], is_transpose=True, start=False, stop=True)
-            assert due == len(marked)
-            return [turn_back(g, GROUP - 1)] + weigh(g)
+                for m in range(MODES):
+                    nc.tensor.matmul(out=w_turned[:], lhsT=y[:, m * C : (m + 1) * C], rhs=ident[:], is_transpose=True, start=False, stop=(m == MODES - 1))
 
-        for unit in stage_a(0):
-            unit()
-        exp_pass(0)
-        softplus_ln_pass(0)
-        ahead = stage_a(1)
-        for unit in ahead[:3]:
-            unit()
-        for unit in interleave(stage_b(0), ahead[3:]):
-            unit()
-        exp_pass(1)
-        belief_ln_pass(0)
-        softplus_ln_pass(1)
-        halve(0)
+            return unit
+
+        def turn_back(g, s):
+            def unit():
+                w_sb = fin.tile([P, P], F32, name="w_sb", tag="w_sb")
+                nc.scalar.copy(out=w_sb[:], in_=w_turned_of[(g, s)][:])
+                if s % QUAD == 0:
+                    w_of[(g, s // QUAD)] = psum_wb.tile([P, QUAD, C], F32, name="w_q", tag="w")
+                nc.tensor.transpose(w_of[(g, s // QUAD)][:, s % QUAD, :], w_sb[:], ident[:])
+
+            return unit
+
+        def weigh(g, h):
+            kept = {}
+            x_quad = x_of[g][:, QUAD * h * C : QUAD * (h + 1) * C]
+            first = GROUP * g + QUAD * h
+
+            def times_g():
+                kept["u"] = fin.tile([P, QUAD * C], F32, name="u_q", tag="u")
+                nc.vector.scalar_tensor_tensor(out=kept["u"][:], in0=x_quad, scalar=EPS, in1=flat(w_of[(g, h)][:]), op0=ALU.add, op1=ALU.mult)
+
+            def minus_eps_j():
+                nc.vector.tensor_tensor(out=kept["u"][:], in0=kept["u"][:], in1=flat(eps_j[:]), op=ALU.subtract)
+
+            def times_x():
+                nc.vector.tensor_tensor(out=kept["u"][:], in0=kept["u"][:], in1=x_quad, op=ALU.mult)
+
+            def sum_up():
+                for t in range(QUAD):
+                    unused = fin.tile([P, C], F32, name="unused", tag="unused")
+                    nc.scalar.activation(out=unused[:], in_=kept["u"][:, t * C : (t + 1) * C], func=ACT.Copy, accum_out=dissonance[:, first + t : first + t + 1])
+
+            return [times_g, minus_eps_j, times_x, sum_up]
+
+        def spread(units, start, end):
+            return [(start + (end - start) * pos / max(len(units) - 1, 1), units[pos]) for pos in range(len(units))]
+
+        def write(chain, marked):
+            marked = sorted(marked, key=lambda pair: pair[0])
+            due = 0
+            for pos in range(len(chain)):
+                chain[pos]()
+                while due < len(marked) and marked[due][0] * len(chain) <= pos + 1:
+                    marked[due][1]()
+                    due += 1
+            for pair in marked[due:]:
+                pair[1]()
+
+        late = []
         carried = []
-        for g in range(GROUPS):
-            chain = stage_b(g + 1) if g + 1 < GROUPS else []
-            feed = stage_a(g + 2) if g + 2 < GROUPS else []
-            carried = rows_of_group(g, chain, feed, carried)
-            if g + 2 < GROUPS:
-                exp_pass(g + 2)
-            if g + 1 < GROUPS:
-                belief_ln_pass(g + 1)
-            if g + 2 < GROUPS:
-                softplus_ln_pass(g + 2)
-            if g + 1 < GROUPS:
-                halve(g + 1)
-
-        cross = const.tile([P, TILES], F32, name="cross")
-        nc.vector.scalar_tensor_tensor(out=cross[:], in0=sum_low[:], scalar=2.0, in1=sum_high[:], op0=ALU.mult, op1=ALU.add)
-        nc.vector.tensor_tensor(out=cross[:], in0=cross[:], in1=sum_high[:], op=ALU.mult)
-        for unit in carried:
-            unit()
-        nc.vector.tensor_tensor(out=dissonance[:], in0=cross[:], in1=weighted[:], op=ALU.add)
+        for p in range(-2, GROUPS):
+            sorting, feeding = p + 1, p + 2
+            if p >= 0:
+                for s in range(GROUP):
+                    belief(p, s)
+                ln_belief(p)
+            if 0 <= sorting < GROUPS:
+                ln_softplus(sorting)
+            feed_units = feed(feeding) if feeding < GROUPS else []
+            if p >= -1 and not late:
+                late = feed_units[:LEAD]
+                feed_units = feed_units[LEAD:]
+            for unit in late:
+                unit()
+            if p == -1:
+                constants()
+            if p >= 0:
+                steps_of_l(p)
+            marked = carried + spread(feed_units, FEED_FROM, FEED_TO)
+            late, carried, chain = [], [], []
+            if 0 <= sorting < GROUPS:
+                evidence(sorting)
+                chain = sort_chain(sorting, 1 if 0 < sorting < GROUPS - 1 else 2)
+                marked += spread([alpha(sorting, s) for s in range(GROUP)], 0.32, 0.40)
+                marked += [(0.45, reciprocal(sorting))]
+                marked += spread([prob(sorting, s) for s in range(GROUP)], 0.50, 0.58)
+            if p >= 0:
+                marked += spread([power(p, h, m) for h in range(QUADS) for m in range(MODES)], 0.0, POWERS_TO)
+                early = GROUP - LATE_SCANS
+                scans = spread([scan(p, s) for s in range(early)], SCANS_FROM, SCANS_TO)
+                marked += scans
+                marked += [(scans[s][0] + AFTER_SCAN, turn_back(p, s)) for s in range(early)]
+                marked += spread(weigh(p, 0), scans[QUAD - 1][0] + 2 * AFTER_SCAN, 0.98)
+                late = [scan(p, s) for s in range(early, GROUP)]
+                carried = spread([turn_back(p, s) for s in range(early, GROUP)], 0.0, 0.04) + spread(weigh(p, 1), 0.08, 0.29)
+            write(chain, marked)
+        write(late, [])
+        write([], carried)
         nc.sync.dma_start(out=vacuity_hbm, in_=vacuity[:])
         nc.sync.dma_start(out=dissonance_hbm, in_=dissonance[:])

@@ -48,12 +48,14 @@ def flat(ap):
     return ap.rearrange("p t c -> p (t c)")
 
 
-LEAD = 3
 LATE_SCANS = 2
-FEED_FROM, FEED_TO = 0.03, 0.86
-POWERS_TO = 0.30
-SCANS_FROM, SCANS_TO = 0.34, 0.89
-AFTER_SCAN = 0.05
+TURN_FROM, TURN_TO = 0.05, 0.62
+QUANT_FROM, QUANT_TO = 0.30, 0.93
+POWERS_TO = 0.02
+SCANS_FROM, SCANS_TO = 0.14, 0.80
+LEAD = 3
+ALPHA_FROM, PROB_FROM = 0.20, 0.45
+CARRY_FROM, CARRY_TO = 0.04, 0.10
 
 
 def tile_evidentialhead_pb_kernel(tc, h_act_bytes, h_act_scale, W3, b3, out_0, out_1, out_2, out_3, out_4):
@@ -70,7 +72,7 @@ def tile_evidentialhead_pb_kernel(tc, h_act_bytes, h_act_scale, W3, b3, out_0, o
         psum_t = ctx.enter_context(tc.psum_pool(name="psum_t", bufs=2))
         psum_acc = ctx.enter_context(tc.psum_pool(name="psum_acc", bufs=2))
         psum_w = ctx.enter_context(tc.psum_pool(name="psum_w", bufs=2))
-        psum_wb = ctx.enter_context(tc.psum_pool(name="psum_wb", bufs=2))
+        psum_one = ctx.enter_context(tc.psum_pool(name="psum_one", bufs=1))
 
         bytes_hbm = h_act_bytes.rearrange("(p t) k -> p t k", t=TILES)
         alpha_hbm = out_0.rearrange("(p t) c -> p t c", t=TILES)
@@ -81,9 +83,11 @@ def tile_evidentialhead_pb_kernel(tc, h_act_bytes, h_act_scale, W3, b3, out_0, o
 
         hbytes = const.tile([P, TILES, K], U8, name="hbytes")
         scale_bc = const.tile([P, K], F32, name="scale_bc")
+        scale_col = const.tile([P, PASSES, 4], F32, name="scale_col")
         w_raw = const.tile([P, PASSES, 4, C], BF16, name="w_raw")
         bias_bc = const.tile([P, C], BF16, name="bias_bc")
         nc.scalar.dma_start(out=scale_bc[:], in_=h_act_scale.rearrange("o k -> (o k)").partition_broadcast(P))
+        nc.scalar.dma_start(out=scale_col[:], in_=h_act_scale.rearrange("o (q p t) -> p (o q) t", p=P, t=4))
         nc.sync.dma_start(out=hbytes[:, 0:FIRST_LOAD, :], in_=bytes_hbm[:, 0:FIRST_LOAD, :])
         nc.sync.dma_start(out=w_raw[:], in_=W3.rearrange("(q p j) n -> p q j n", p=P, j=4))
         nc.sync.dma_start(out=bias_bc[:], in_=b3.partition_broadcast(P))
@@ -97,6 +101,8 @@ def tile_evidentialhead_pb_kernel(tc, h_act_bytes, h_act_scale, W3, b3, out_0, o
         make_identity(nc, ident[:])
         index_i = const.tile([P, C], I32, name="index_i")
         nc.gpsimd.iota(out=index_i[:], pattern=[[1, C]], base=0, channel_multiplier=0)
+        partition_i = const.tile([P, 1], I32, name="partition_i")
+        nc.gpsimd.iota(out=partition_i[:], pattern=[[0, 1]], base=0, channel_multiplier=1)
         lam = [const.tile([P, GROUP, C], F32, name="lam0"), const.tile([P, GROUP, C], F32, name="lam1")]
         for lam_tile in lam:
             nc.gpsimd.memset(lam_tile[:], RESET)
@@ -120,36 +126,42 @@ def tile_evidentialhead_pb_kernel(tc, h_act_bytes, h_act_scale, W3, b3, out_0, o
 
         j_row = const.tile([P, C], F32, name="j_row")
         a_row = const.tile([P, C], F32, name="a_row")
-        eps_j = const.tile([P, QUAD, C], F32, name="eps_j")
+        eps_j = const.tile([P, 1], F32, name="eps_j")
         c_rows = const.tile([P, MODES, C], F32, name="c_rows")
 
         def constants():
             nc.vector.tensor_copy(out=j_row[:], in_=index_i[:])
             nc.vector.tensor_scalar(out=a_row[:], in0=j_row[:], scalar1=CONSTANT, scalar2=-sum(WEIGHTS), op0=ALU.mult, op1=ALU.add)
-            for s in range(QUAD):
-                nc.vector.tensor_scalar(out=eps_j[:, s, :], in0=j_row[:], scalar1=EPS, scalar2=None, op0=ALU.mult)
+            nc.vector.tensor_copy(out=eps_j[:], in_=partition_i[:])
+            nc.vector.tensor_scalar(out=eps_j[:], in0=eps_j[:], scalar1=EPS, scalar2=None, op0=ALU.mult)
             for m in range(MODES):
                 nc.vector.tensor_scalar(out=c_rows[:, m, :], in0=zeros[:], scalar1=WEIGHTS[m], scalar2=None, op0=ALU.add)
 
         vacuity = const.tile([P, TILES], F32, name="vacuity")
         dissonance = const.tile([P, TILES], F32, name="dissonance")
+        dissonance_ps = psum_one.tile([P, TILES], F32, name="dissonance_ps", tag="dissonance_ps")
 
         logit_of = [None] * GROUPS
         soft_of = [None] * GROUPS
         sorted_of = [None] * GROUPS
         rs_of = [None] * GROUPS
         x_of = [None] * GROUPS
+        xt_of = [None] * GROUPS
         e_of = {}
 
         def feed(g):
             turned_of, grouped_of, acc_of = {}, {}, {}
+            by_vector = GROUP if g == 0 else (LEAD if g <= 2 else 0)
 
             def widen(s):
                 if s == 0:
                     logit_of[g] = grp.tile([P, GROUP, C], F32, name="logit_g", tag="logit")
                     soft_of[g] = grp.tile([P, GROUP, C], F32, name="soft_g", tag="soft")
                 h_bf = stage.tile([P, K], BF16, name="h_bf", tag="h_bf", align_bytes=64)
-                nc.vector.tensor_tensor(out=h_bf[:], in0=hbytes[:, GROUP * g + s, :].bitcast(FP8), in1=scale_bc[:], op=ALU.mult)
+                if s < by_vector:
+                    nc.vector.tensor_tensor(out=h_bf[:], in0=hbytes[:, GROUP * g + s, :].bitcast(FP8), in1=scale_bc[:], op=ALU.mult)
+                else:
+                    nc.scalar.copy(out=h_bf[:], in_=hbytes[:, GROUP * g + s, :].bitcast(FP8))
                 words = h_bf[:].bitcast(F32)
                 turned = psum_t.tile([P, PASSES, 2, P], F32, name="turned", tag="turned")
                 for q in range(PASSES):
@@ -158,8 +170,17 @@ def tile_evidentialhead_pb_kernel(tc, h_act_bytes, h_act_scale, W3, b3, out_0, o
                 turned_of[s] = turned
 
             def copy_out(s):
-                grouped = stage.tile([P, PASSES, P, 4], BF16, name="grouped", tag="grouped", align_bytes=64)
-                nc.scalar.copy(out=grouped[:].bitcast(F32), in_=turned_of[s][:].rearrange("p q u r -> p q r u"))
+                grouped = stage.tile([P, PASSES, P, 4], BF16, name="grouped", tag="grouped", align_bytes=64, bufs=GROUP)
+                if s < by_vector:
+                    nc.scalar.copy(out=grouped[:].bitcast(F32), in_=turned_of[s][:].rearrange("p q u r -> p q r u"))
+                else:
+                    halves = turned_of[s][:].bitcast(BF16).rearrange("p q u (r e) -> p q u r e", e=2)
+                    scaled = stage.tile([P, PASSES, 2, P, 2], BF16, name="scaled", tag="scaled")
+                    for q in range(PASSES):
+                        for u in range(2):
+                            for e in range(2):
+                                nc.scalar.activation(out=scaled[:, q, u, :, e], in_=halves[:, q, u, :, e], func=ACT.Copy, scale=scale_col[:, q, 2 * u + e : 2 * u + e + 1])
+                    nc.scalar.copy(out=grouped[:].bitcast(F32), in_=scaled[:].rearrange("p q u r e -> p q u (r e)").bitcast(F32).rearrange("p q u r -> p q r u"))
                 grouped_of[s] = grouped
 
             def quantise(s):
@@ -188,22 +209,27 @@ def tile_evidentialhead_pb_kernel(tc, h_act_bytes, h_act_scale, W3, b3, out_0, o
                 nc.scalar.activation(out=soft_of[g][:, tiles, :], in_=logit_of[g][:, tiles, :], func=ACT.Abs)
                 nc.scalar.activation(out=soft_of[g][:, tiles, :], in_=soft_of[g][:, tiles, :], func=ACT.Exp, scale=-1.0)
 
-            def step(i):
+            def scalar_step(i):
                 def unit():
                     if i < GROUP:
                         widen(i)
-                    if 1 <= i <= GROUP:
+                    if i >= 1:
                         copy_out(i - 1)
-                    if 2 <= i <= GROUP + 1:
-                        quantise(i - 2)
-                    if i >= 3 and (i - 3) % QUAD == QUAD - 1:
-                        add_bias((i - 3) // QUAD)
-                    if i >= 4 and (i - 4) % QUAD == QUAD - 1:
-                        abs_exp((i - 4) // QUAD)
 
                 return unit
 
-            return [step(i) for i in range(GROUP + 4)]
+            def vector_step(i):
+                def unit():
+                    if i < GROUP:
+                        quantise(i)
+                    if i % QUAD == 0 and i > 0:
+                        add_bias(i // QUAD - 1)
+                    if i % QUAD == 1 and i > 1:
+                        abs_exp(i // QUAD - 1)
+
+                return unit
+
+            return [scalar_step(i) for i in range(GROUP + 1)], [vector_step(i) for i in range(GROUP + 2)]
 
         held = [dict() for g in range(GROUPS)]
 
@@ -304,12 +330,22 @@ def tile_evidentialhead_pb_kernel(tc, h_act_bytes, h_act_scale, W3, b3, out_0, o
 
             return unit
 
-        w_turned_of = {}
-        w_of = {}
+        def turn_beliefs(g, h):
+            def unit():
+                xt_ps = psum_one.tile([P, QUAD, P], F32, name="xt_ps", tag="xt_ps")
+                for s in range(QUAD):
+                    nc.tensor.transpose(xt_ps[:, s, :], x_of[g][:, (QUAD * h + s) * C : (QUAD * h + s + 1) * C], ident[:])
+                if h == 0:
+                    xt_of[g] = sortp.tile([P, GROUP, P], F32, name="xt_g", tag="xt", bufs=2)
+                nc.scalar.copy(out=xt_of[g][:, QUAD * h : QUAD * (h + 1), :], in_=xt_ps[:])
+
+            return unit
+
+        g_of = {}
 
         def scan(g, s):
             def unit():
-                y = modes.tile([P, MODES * C], F32, name="y_t", tag="y", bufs=3)
+                y = modes.tile([P, MODES * C], F32, name="y_t", tag="y", bufs=4)
                 nc.vector.tensor_tensor_scan(
                     out=y[:],
                     data0=e_of[(g, s // QUAD)][:, s % QUAD, :, :].rearrange("p k j -> p (k j)"),
@@ -318,45 +354,29 @@ def tile_evidentialhead_pb_kernel(tc, h_act_bytes, h_act_scale, W3, b3, out_0, o
                     op0=ALU.mult,
                     op1=ALU.add,
                 )
-                w_turned = psum_w.tile([P, P], F32, name="w_turned", tag="w_turned")
-                w_turned_of[(g, s)] = w_turned
-                nc.tensor.matmul(out=w_turned[:], lhsT=a_row[:], rhs=ident[:], is_transpose=True, start=True, stop=False)
-                for m in range(MODES):
-                    nc.tensor.matmul(out=w_turned[:], lhsT=y[:, m * C : (m + 1) * C], rhs=ident[:], is_transpose=True, start=False, stop=(m == MODES - 1))
-
-            return unit
-
-        def turn_back(g, s):
-            def unit():
-                w_sb = fin.tile([P, P], F32, name="w_sb", tag="w_sb")
-                nc.scalar.copy(out=w_sb[:], in_=w_turned_of[(g, s)][:])
                 if s % QUAD == 0:
-                    w_of[(g, s // QUAD)] = psum_wb.tile([P, QUAD, C], F32, name="w_q", tag="w")
-                nc.tensor.transpose(w_of[(g, s // QUAD)][:, s % QUAD, :], w_sb[:], ident[:])
+                    g_of[(g, s // QUAD)] = psum_w.tile([P, QUAD, P], F32, name="g_q", tag="g_q")
+                g_turned = g_of[(g, s // QUAD)][:, s % QUAD, :]
+                nc.tensor.matmul(out=g_turned, lhsT=a_row[:], rhs=ident[:], is_transpose=True, start=True, stop=False)
+                for m in range(MODES):
+                    nc.tensor.matmul(out=g_turned, lhsT=y[:, m * C : (m + 1) * C], rhs=ident[:], is_transpose=True, start=False, stop=(m == MODES - 1))
 
             return unit
 
         def weigh(g, h):
             kept = {}
-            x_quad = x_of[g][:, QUAD * h * C : QUAD * (h + 1) * C]
             first = GROUP * g + QUAD * h
 
             def times_g():
-                kept["u"] = fin.tile([P, QUAD * C], F32, name="u_q", tag="u")
-                nc.vector.scalar_tensor_tensor(out=kept["u"][:], in0=x_quad, scalar=EPS, in1=flat(w_of[(g, h)][:]), op0=ALU.add, op1=ALU.mult)
-
-            def minus_eps_j():
-                nc.vector.tensor_tensor(out=kept["u"][:], in0=kept["u"][:], in1=flat(eps_j[:]), op=ALU.subtract)
+                kept["u"] = fin.tile([P, QUAD, P], F32, name="u_q", tag="u")
+                nc.vector.scalar_tensor_tensor(out=flat(kept["u"][:]), in0=flat(xt_of[g][:, QUAD * h : QUAD * (h + 1), :]), scalar=EPS, in1=flat(g_of[(g, h)][:]), op0=ALU.add, op1=ALU.mult)
 
             def times_x():
-                nc.vector.tensor_tensor(out=kept["u"][:], in0=kept["u"][:], in1=x_quad, op=ALU.mult)
+                nc.vector.scalar_tensor_tensor(out=flat(kept["u"][:]), in0=flat(kept["u"][:]), scalar=eps_j[:], in1=flat(xt_of[g][:, QUAD * h : QUAD * (h + 1), :]), op0=ALU.subtract, op1=ALU.mult)
+                for s in range(QUAD):
+                    nc.tensor.matmul(out=dissonance_ps[:, first + s : first + s + 1], lhsT=kept["u"][:, s, :], rhs=one_col[:], start=True, stop=True)
 
-            def sum_up():
-                for t in range(QUAD):
-                    unused = fin.tile([P, C], F32, name="unused", tag="unused")
-                    nc.scalar.activation(out=unused[:], in_=kept["u"][:, t * C : (t + 1) * C], func=ACT.Copy, accum_out=dissonance[:, first + t : first + t + 1])
-
-            return [times_g, minus_eps_j, times_x, sum_up]
+            return [times_g, times_x]
 
         def spread(units, start, end):
             return [(start + (end - start) * pos / max(len(units) - 1, 1), units[pos]) for pos in range(len(units))]
@@ -382,35 +402,41 @@ def tile_evidentialhead_pb_kernel(tc, h_act_bytes, h_act_scale, W3, b3, out_0, o
                 ln_belief(p)
             if 0 <= sorting < GROUPS:
                 ln_softplus(sorting)
-            feed_units = feed(feeding) if feeding < GROUPS else []
+            turn_units, quant_units = feed(feeding) if feeding < GROUPS else ([], [])
             if p >= -1 and not late:
-                late = feed_units[:LEAD]
-                feed_units = feed_units[LEAD:]
-            for unit in late:
+                late = turn_units[:LEAD]
+                turn_units = turn_units[LEAD:]
+            for unit in late[:LATE_SCANS]:
                 unit()
             if p == -1:
                 constants()
             if p >= 0:
                 steps_of_l(p)
-            marked = carried + spread(feed_units, FEED_FROM, FEED_TO)
+            for unit in late[LATE_SCANS:]:
+                unit()
+            marked = carried + spread(turn_units, TURN_FROM, TURN_TO) + spread(quant_units, QUANT_FROM, QUANT_TO)
             late, carried, chain = [], [], []
             if 0 <= sorting < GROUPS:
                 evidence(sorting)
-                chain = sort_chain(sorting, 1 if 0 < sorting < GROUPS - 1 else 2)
-                marked += spread([alpha(sorting, s) for s in range(GROUP)], 0.32, 0.40)
-                marked += [(0.45, reciprocal(sorting))]
-                marked += spread([prob(sorting, s) for s in range(GROUP)], 0.50, 0.58)
+                chain = sort_chain(sorting, 2)
+                marked += spread([alpha(sorting, s) for s in range(GROUP)], ALPHA_FROM, ALPHA_FROM + 0.04)
+                marked += [(PROB_FROM - 0.05, reciprocal(sorting))]
+                marked += spread([prob(sorting, s) for s in range(GROUP)], PROB_FROM, PROB_FROM + 0.04)
             if p >= 0:
                 marked += spread([power(p, h, m) for h in range(QUADS) for m in range(MODES)], 0.0, POWERS_TO)
-                early = GROUP - LATE_SCANS
+                early = GROUP - (LATE_SCANS if sorting < GROUPS - 1 else 2 * LATE_SCANS)
                 scans = spread([scan(p, s) for s in range(early)], SCANS_FROM, SCANS_TO)
                 marked += scans
-                marked += [(scans[s][0] + AFTER_SCAN, turn_back(p, s)) for s in range(early)]
-                marked += spread(weigh(p, 0), scans[QUAD - 1][0] + 2 * AFTER_SCAN, 0.98)
+                marked += spread([turn_beliefs(p, h) for h in range(QUADS)], POWERS_TO + 0.01, POWERS_TO + 0.02)
                 late = [scan(p, s) for s in range(early, GROUP)]
-                carried = spread([turn_back(p, s) for s in range(early, GROUP)], 0.0, 0.04) + spread(weigh(p, 1), 0.08, 0.29)
+                if early > QUAD:
+                    marked += spread(weigh(p, 0), scans[QUAD][0] + 0.03, scans[QUAD][0] + 0.08)
+                else:
+                    late = late[:LATE_SCANS] + weigh(p, 0) + late[LATE_SCANS:]
+                carried = spread(weigh(p, 1), CARRY_FROM, CARRY_TO)
             write(chain, marked)
         write(late, [])
         write([], carried)
         nc.sync.dma_start(out=vacuity_hbm, in_=vacuity[:])
+        nc.vector.tensor_copy(out=dissonance[:], in_=dissonance_ps[:])
         nc.sync.dma_start(out=dissonance_hbm, in_=dissonance[:])

@@ -48,13 +48,14 @@ def flat(ap):
     return ap.rearrange("p t c -> p (t c)")
 
 
+KEPT = 3
 LATE_SCANS = 2
 TURN_FROM, TURN_TO = 0.05, 0.62
-QUANT_FROM, QUANT_TO = 0.30, 0.93
+QUANT_FROM, QUANT_TO = 0.38, 0.96
 POWERS_TO = 0.02
-SCANS_FROM, SCANS_TO = 0.14, 0.80
+SCANS_FROM, SCANS_TO = 0.16, 0.80
 LEAD = 3
-ALPHA_FROM, PROB_FROM = 0.20, 0.45
+ALPHA_FROM, PROB_FROM = 0.20, 0.62
 CARRY_FROM, CARRY_TO = 0.04, 0.10
 
 
@@ -70,9 +71,10 @@ def tile_evidentialhead_pb_kernel(tc, h_act_bytes, h_act_scale, W3, b3, out_0, o
         modes = ctx.enter_context(tc.tile_pool(name="modes", bufs=2))
         fin = ctx.enter_context(tc.tile_pool(name="fin", bufs=2))
         psum_t = ctx.enter_context(tc.psum_pool(name="psum_t", bufs=2))
-        psum_acc = ctx.enter_context(tc.psum_pool(name="psum_acc", bufs=2))
+        psum_acc = ctx.enter_context(tc.psum_pool(name="psum_acc", bufs=1))
         psum_w = ctx.enter_context(tc.psum_pool(name="psum_w", bufs=2))
         psum_one = ctx.enter_context(tc.psum_pool(name="psum_one", bufs=1))
+        psum_back = ctx.enter_context(tc.psum_pool(name="psum_back", bufs=2))
 
         bytes_hbm = h_act_bytes.rearrange("(p t) k -> p t k", t=TILES)
         alpha_hbm = out_0.rearrange("(p t) c -> p t c", t=TILES)
@@ -111,13 +113,18 @@ def tile_evidentialhead_pb_kernel(tc, h_act_bytes, h_act_scale, W3, b3, out_0, o
         nc.scalar.activation(out=warm[:], in_=zeros[:, 0:1], func=ACT.Exp)
 
         w_grouped = const.tile([P, PASSES, C, 4], BF16, name="w_grouped", align_bytes=64)
-        nc.vector.tensor_copy(out=w_grouped[:], in_=w_raw[:].rearrange("p q j n -> p q n j"))
         w_codes = const.tile([P, PASSES * C], U32, name="w_codes", align_bytes=64)
         w_scales = const.tile([P, PASSES * C], U8, name="w_scales", align_bytes=64)
-        bias_quad = const.tile([P, QUAD, C], BF16, name="bias_quad")
-        for s in range(QUAD):
-            nc.vector.tensor_copy(out=bias_quad[:, s, :], in_=bias_bc[:])
-        nc.vector.quantize_mx(out=w_codes[:].bitcast(FP8X4), scales=w_scales[:], in_=w_grouped[:].rearrange("p q n j -> p (q n j)"))
+        bias_rows = const.tile([P, C], F32, name="bias_rows")
+        bias_col = const.tile([P, 1], F32, name="bias_col")
+
+        def weights():
+            nc.vector.tensor_copy(out=w_grouped[:], in_=w_raw[:].rearrange("p q j n -> p q n j"))
+            nc.vector.tensor_copy(out=bias_rows[:], in_=bias_bc[:])
+            bias_turned = psum_back.tile([P, QUAD, P], F32, name="bias_turned", tag="back")
+            nc.tensor.transpose(bias_turned[:, 0, :], bias_rows[:], ident[:])
+            nc.vector.quantize_mx(out=w_codes[:].bitcast(FP8X4), scales=w_scales[:], in_=w_grouped[:].rearrange("p q n j -> p (q n j)"))
+            nc.vector.tensor_copy(out=bias_col[:], in_=bias_turned[:, 0, 0:1])
 
         one_col = const.tile([P, 1], F32, name="one_col")
         nc.vector.memset(one_col[:], 1.0)
@@ -193,20 +200,18 @@ def tile_evidentialhead_pb_kernel(tc, h_act_bytes, h_act_scale, W3, b3, out_0, o
                     cols = slice(P * q, P * (q + 1))
                     nc.tensor.matmul_mx(
                         out=acc_of[s // QUAD][:, s % QUAD, :],
-                        lhsT=codes[:, cols].bitcast(FP8X4),
-                        lhsT_scale=scales[:, cols],
-                        rhs=w_codes[:, cols].bitcast(FP8X4),
-                        rhs_scale=w_scales[:, cols],
+                        lhsT=w_codes[:, cols].bitcast(FP8X4),
+                        lhsT_scale=w_scales[:, cols],
+                        rhs=codes[:, cols].bitcast(FP8X4),
+                        rhs_scale=scales[:, cols],
                         start=(q == 0),
                         stop=(q == PASSES - 1),
                     )
 
-            def add_bias(h):
-                nc.vector.tensor_tensor(out=logit_of[g][:, QUAD * h : QUAD * (h + 1), :], in0=acc_of[h][:], in1=bias_quad[:], op=ALU.add)
-
-            def abs_exp(h):
+            def relu_abs_exp(h):
                 tiles = slice(QUAD * h, QUAD * (h + 1))
-                nc.scalar.activation(out=soft_of[g][:, tiles, :], in_=logit_of[g][:, tiles, :], func=ACT.Abs)
+                nc.scalar.activation(out=soft_of[g][:, tiles, :], in_=acc_of[h][:], func=ACT.Abs, bias=bias_col[:])
+                nc.scalar.activation(out=logit_of[g][:, tiles, :], in_=acc_of[h][:], func=ACT.Relu, bias=bias_col[:])
                 nc.scalar.activation(out=soft_of[g][:, tiles, :], in_=soft_of[g][:, tiles, :], func=ACT.Exp, scale=-1.0)
 
             def scalar_step(i):
@@ -220,27 +225,33 @@ def tile_evidentialhead_pb_kernel(tc, h_act_bytes, h_act_scale, W3, b3, out_0, o
 
             def vector_step(i):
                 def unit():
+                    if i % QUAD == 0 and i > 0:
+                        relu_abs_exp(i // QUAD - 1)
                     if i < GROUP:
                         quantise(i)
-                    if i % QUAD == 0 and i > 0:
-                        add_bias(i // QUAD - 1)
-                    if i % QUAD == 1 and i > 1:
-                        abs_exp(i // QUAD - 1)
 
                 return unit
 
-            return [scalar_step(i) for i in range(GROUP + 1)], [vector_step(i) for i in range(GROUP + 2)]
+            return [scalar_step(i) for i in range(GROUP + 1)], [vector_step(i) for i in range(GROUP + 1)]
 
         held = [dict() for g in range(GROUPS)]
 
         def ln_softplus(g):
             nc.scalar.activation(out=flat(soft_of[g][:]), in_=flat(soft_of[g][:]), func=ACT.Ln, bias=one_col[:])
 
-        def evidence(g):
-            tiles = slice(GROUP * g, GROUP * (g + 1))
-            held[g]["ev"] = outp.tile([P, GROUP, C], F32, name="ev_g", tag="ev")
-            nc.vector.scalar_tensor_tensor(out=flat(held[g]["ev"][:]), in0=flat(logit_of[g][:]), scalar=0.0, in1=flat(soft_of[g][:]), op0=ALU.max, op1=ALU.add)
-            nc.sync.dma_start(out=evidence_hbm[:, tiles, :], in_=held[g]["ev"][:])
+        def evidence_turn(g, h):
+            held[g][("ev_ps", h)] = psum_back.tile([P, QUAD, C], F32, name="ev_ps", tag="back")
+            for s in range(QUAD):
+                out = held[g][("ev_ps", h)][:, s, :]
+                nc.tensor.matmul(out=out, lhsT=logit_of[g][:, QUAD * h + s, :], rhs=ident[:], is_transpose=True, start=True, stop=False)
+                nc.tensor.matmul(out=out, lhsT=soft_of[g][:, QUAD * h + s, :], rhs=ident[:], is_transpose=True, start=False, stop=True)
+
+        def evidence_copy(g, h):
+            if h == 0:
+                held[g]["ev"] = outp.tile([P, GROUP, C], F32, name="ev_g", tag="ev")
+            nc.scalar.copy(out=held[g]["ev"][:, QUAD * h : QUAD * (h + 1), :], in_=held[g][("ev_ps", h)][:])
+            if h == QUADS - 1:
+                nc.sync.dma_start(out=evidence_hbm[:, GROUP * g : GROUP * (g + 1), :], in_=held[g]["ev"][:])
 
         def alpha(g, s):
             def unit():
@@ -257,6 +268,11 @@ def tile_evidentialhead_pb_kernel(tc, h_act_bytes, h_act_scale, W3, b3, out_0, o
             def unit():
                 rs_of[g] = fin.tile([P, GROUP], F32, name="rs_g", tag="rS")
                 nc.vector.reciprocal(out=rs_of[g][:], in_=held[g]["S"][:])
+
+            return unit
+
+        def vacuity_of(g):
+            def unit():
                 nc.vector.tensor_scalar(out=vacuity[:, GROUP * g : GROUP * (g + 1)], in0=rs_of[g][:], scalar1=float(C), scalar2=None, op0=ALU.mult)
 
             return unit
@@ -332,7 +348,7 @@ def tile_evidentialhead_pb_kernel(tc, h_act_bytes, h_act_scale, W3, b3, out_0, o
 
         def turn_beliefs(g, h):
             def unit():
-                xt_ps = psum_one.tile([P, QUAD, P], F32, name="xt_ps", tag="xt_ps")
+                xt_ps = psum_back.tile([P, QUAD, P], F32, name="xt_ps", tag="back")
                 for s in range(QUAD):
                     nc.tensor.transpose(xt_ps[:, s, :], x_of[g][:, (QUAD * h + s) * C : (QUAD * h + s + 1) * C], ident[:])
                 if h == 0:
@@ -396,12 +412,17 @@ def tile_evidentialhead_pb_kernel(tc, h_act_bytes, h_act_scale, W3, b3, out_0, o
         carried = []
         for p in range(-2, GROUPS):
             sorting, feeding = p + 1, p + 2
+            if 0 <= sorting < GROUPS:
+                ln_softplus(sorting)
+                for h in range(QUADS):
+                    evidence_turn(sorting, h)
             if p >= 0:
                 for s in range(GROUP):
                     belief(p, s)
                 ln_belief(p)
             if 0 <= sorting < GROUPS:
-                ln_softplus(sorting)
+                for h in range(QUADS):
+                    evidence_copy(sorting, h)
             turn_units, quant_units = feed(feeding) if feeding < GROUPS else ([], [])
             if p >= -1 and not late:
                 late = turn_units[:LEAD]
@@ -415,16 +436,17 @@ def tile_evidentialhead_pb_kernel(tc, h_act_bytes, h_act_scale, W3, b3, out_0, o
             for unit in late[LATE_SCANS:]:
                 unit()
             marked = carried + spread(turn_units, TURN_FROM, TURN_TO) + spread(quant_units, QUANT_FROM, QUANT_TO)
+            if p == -2:
+                marked += [(TURN_FROM + 0.1, weights)]
             late, carried, chain = [], [], []
             if 0 <= sorting < GROUPS:
-                evidence(sorting)
                 chain = sort_chain(sorting, 2)
                 marked += spread([alpha(sorting, s) for s in range(GROUP)], ALPHA_FROM, ALPHA_FROM + 0.04)
-                marked += [(PROB_FROM - 0.05, reciprocal(sorting))]
+                marked += [(PROB_FROM - 0.05, reciprocal(sorting)), (PROB_FROM, vacuity_of(sorting))]
                 marked += spread([prob(sorting, s) for s in range(GROUP)], PROB_FROM, PROB_FROM + 0.04)
             if p >= 0:
                 marked += spread([power(p, h, m) for h in range(QUADS) for m in range(MODES)], 0.0, POWERS_TO)
-                early = GROUP - (LATE_SCANS if sorting < GROUPS - 1 else 2 * LATE_SCANS)
+                early = GROUP - (KEPT if sorting < GROUPS - 1 else QUAD)
                 scans = spread([scan(p, s) for s in range(early)], SCANS_FROM, SCANS_TO)
                 marked += scans
                 marked += spread([turn_beliefs(p, h) for h in range(QUADS)], POWERS_TO + 0.01, POWERS_TO + 0.02)
@@ -432,7 +454,7 @@ def tile_evidentialhead_pb_kernel(tc, h_act_bytes, h_act_scale, W3, b3, out_0, o
                 if early > QUAD:
                     marked += spread(weigh(p, 0), scans[QUAD][0] + 0.03, scans[QUAD][0] + 0.08)
                 else:
-                    late = late[:LATE_SCANS] + weigh(p, 0) + late[LATE_SCANS:]
+                    late = late[:LATE_SCANS] + [unit for pair in zip(weigh(p, 0), late[LATE_SCANS:]) for unit in pair]
                 carried = spread(weigh(p, 1), CARRY_FROM, CARRY_TO)
             write(chain, marked)
         write(late, [])

@@ -56,7 +56,8 @@ POWERS_TO = 0.02
 SCANS_FROM, SCANS_TO = 0.16, 0.80
 LEAD = 3
 ALPHA_FROM, PROB_FROM = 0.20, 0.62
-CARRY_FROM, CARRY_TO = 0.04, 0.10
+CARRY_FROM, CARRY_TO = 0.18, 0.24
+COLLECT_FIRST, COLLECT_SECOND = 0.96, 0.55
 
 
 def tile_evidentialhead_pb_kernel(tc, h_act_bytes, h_act_scale, W3, b3, out_0, out_1, out_2, out_3, out_4):
@@ -71,9 +72,8 @@ def tile_evidentialhead_pb_kernel(tc, h_act_bytes, h_act_scale, W3, b3, out_0, o
         modes = ctx.enter_context(tc.tile_pool(name="modes", bufs=2))
         fin = ctx.enter_context(tc.tile_pool(name="fin", bufs=2))
         psum_t = ctx.enter_context(tc.psum_pool(name="psum_t", bufs=2))
-        psum_acc = ctx.enter_context(tc.psum_pool(name="psum_acc", bufs=1))
+        psum_acc = ctx.enter_context(tc.psum_pool(name="psum_acc", bufs=2))
         psum_w = ctx.enter_context(tc.psum_pool(name="psum_w", bufs=2))
-        psum_one = ctx.enter_context(tc.psum_pool(name="psum_one", bufs=1))
         psum_back = ctx.enter_context(tc.psum_pool(name="psum_back", bufs=2))
 
         bytes_hbm = h_act_bytes.rearrange("(p t) k -> p t k", t=TILES)
@@ -146,7 +146,6 @@ def tile_evidentialhead_pb_kernel(tc, h_act_bytes, h_act_scale, W3, b3, out_0, o
 
         vacuity = const.tile([P, TILES], F32, name="vacuity")
         dissonance = const.tile([P, TILES], F32, name="dissonance")
-        dissonance_ps = psum_one.tile([P, TILES], F32, name="dissonance_ps", tag="dissonance_ps")
 
         logit_of = [None] * GROUPS
         soft_of = [None] * GROUPS
@@ -191,8 +190,8 @@ def tile_evidentialhead_pb_kernel(tc, h_act_bytes, h_act_scale, W3, b3, out_0, o
                 grouped_of[s] = grouped
 
             def quantise(s):
-                codes = stage.tile([P, PASSES * P], U32, name="codes", tag="codes", align_bytes=64)
-                scales = stage.tile([P, PASSES * P], U8, name="scales", tag="scales", align_bytes=64)
+                codes = stage.tile([P, PASSES * P], U32, name="codes", tag="codes", align_bytes=64, bufs=5)
+                scales = stage.tile([P, PASSES * P], U8, name="scales", tag="scales", align_bytes=64, bufs=5)
                 nc.vector.quantize_mx(out=codes[:].bitcast(FP8X4), scales=scales[:], in_=grouped_of[s][:].rearrange("p q r t -> p (q r t)"))
                 if s % QUAD == 0:
                     acc_of[s // QUAD] = psum_acc.tile([P, QUAD, C], F32, name="acc", tag="acc")
@@ -390,9 +389,12 @@ def tile_evidentialhead_pb_kernel(tc, h_act_bytes, h_act_scale, W3, b3, out_0, o
             def times_x():
                 nc.vector.scalar_tensor_tensor(out=flat(kept["u"][:]), in0=flat(kept["u"][:]), scalar=eps_j[:], in1=flat(xt_of[g][:, QUAD * h : QUAD * (h + 1), :]), op0=ALU.subtract, op1=ALU.mult)
                 for s in range(QUAD):
-                    nc.tensor.matmul(out=dissonance_ps[:, first + s : first + s + 1], lhsT=kept["u"][:, s, :], rhs=one_col[:], start=True, stop=True)
+                    nc.tensor.matmul(out=g_of[(g, h)][:, s, 0:1], lhsT=kept["u"][:, s, :], rhs=one_col[:], start=True, stop=True)
 
-            return [times_g, times_x]
+            def collect():
+                nc.vector.tensor_copy(out=dissonance[:, first : first + QUAD], in_=g_of[(g, h)][:, :, 0])
+
+            return [times_g, times_x, collect]
 
         def spread(units, start, end):
             return [(start + (end - start) * pos / max(len(units) - 1, 1), units[pos]) for pos in range(len(units))]
@@ -452,13 +454,15 @@ def tile_evidentialhead_pb_kernel(tc, h_act_bytes, h_act_scale, W3, b3, out_0, o
                 marked += spread([turn_beliefs(p, h) for h in range(QUADS)], POWERS_TO + 0.01, POWERS_TO + 0.02)
                 late = [scan(p, s) for s in range(early, GROUP)]
                 if early > QUAD:
-                    marked += spread(weigh(p, 0), scans[QUAD][0] + 0.03, scans[QUAD][0] + 0.08)
+                    first_quad = weigh(p, 0)
+                    marked += spread(first_quad[:2], scans[QUAD][0] + 0.03, scans[QUAD][0] + 0.08) + [(COLLECT_FIRST, first_quad[2])]
                 else:
-                    late = late[:LATE_SCANS] + [unit for pair in zip(weigh(p, 0), late[LATE_SCANS:]) for unit in pair]
-                carried = spread(weigh(p, 1), CARRY_FROM, CARRY_TO)
+                    first_quad = weigh(p, 0)
+                    late = late[:LATE_SCANS] + [first_quad[0], late[LATE_SCANS], first_quad[1], late[LATE_SCANS + 1], first_quad[2]]
+                second_quad = weigh(p, 1)
+                carried = spread(second_quad[:2], CARRY_FROM, CARRY_TO) + [(COLLECT_SECOND, second_quad[2])]
             write(chain, marked)
         write(late, [])
         write([], carried)
         nc.sync.dma_start(out=vacuity_hbm, in_=vacuity[:])
-        nc.vector.tensor_copy(out=dissonance[:], in_=dissonance_ps[:])
         nc.sync.dma_start(out=dissonance_hbm, in_=dissonance[:])

@@ -54,9 +54,10 @@ TURN_FROM, TURN_TO = 0.05, 0.62
 QUANT_FROM, QUANT_TO = 0.38, 0.96
 POWERS_TO = 0.02
 SCANS_FROM, SCANS_TO = 0.16, 0.80
+STEADY = 1
 LEAD = 3
 ALPHA_FROM, PROB_FROM = 0.20, 0.62
-CARRY_FROM, CARRY_TO = 0.18, 0.24
+CARRY_FROM = 0.18
 COLLECT_FIRST, COLLECT_SECOND = 0.96, 0.55
 
 
@@ -101,8 +102,6 @@ def tile_evidentialhead_pb_kernel(tc, h_act_bytes, h_act_scale, W3, b3, out_0, o
         nc.gpsimd.memset(zeros[:], 0.0)
         ident = const.tile([P, P], F32, name="ident")
         make_identity(nc, ident[:])
-        index_i = const.tile([P, C], I32, name="index_i")
-        nc.gpsimd.iota(out=index_i[:], pattern=[[1, C]], base=0, channel_multiplier=0)
         partition_i = const.tile([P, 1], I32, name="partition_i")
         nc.gpsimd.iota(out=partition_i[:], pattern=[[0, 1]], base=0, channel_multiplier=1)
         lam = [const.tile([P, GROUP, C], F32, name="lam0"), const.tile([P, GROUP, C], F32, name="lam1")]
@@ -131,16 +130,15 @@ def tile_evidentialhead_pb_kernel(tc, h_act_bytes, h_act_scale, W3, b3, out_0, o
         half_eps_col = const.tile([P, 1], F32, name="half_eps_col")
         nc.vector.tensor_scalar(out=half_eps_col[:], in0=zeros[:, 0:1], scalar1=0.5 * EPS, scalar2=None, op0=ALU.add)
 
-        j_row = const.tile([P, C], F32, name="j_row")
-        a_row = const.tile([P, C], F32, name="a_row")
-        eps_j = const.tile([P, 1], F32, name="eps_j")
+        j_col = const.tile([P, 1], F32, name="j_col")
+        a_col = const.tile([P, 1], F32, name="a_col")
+        minus_eps_j = const.tile([P, 1], F32, name="minus_eps_j")
         c_rows = const.tile([P, MODES, C], F32, name="c_rows")
 
         def constants():
-            nc.vector.tensor_copy(out=j_row[:], in_=index_i[:])
-            nc.vector.tensor_scalar(out=a_row[:], in0=j_row[:], scalar1=CONSTANT, scalar2=-sum(WEIGHTS), op0=ALU.mult, op1=ALU.add)
-            nc.vector.tensor_copy(out=eps_j[:], in_=partition_i[:])
-            nc.vector.tensor_scalar(out=eps_j[:], in0=eps_j[:], scalar1=EPS, scalar2=None, op0=ALU.mult)
+            nc.vector.tensor_copy(out=j_col[:], in_=partition_i[:])
+            nc.vector.tensor_scalar(out=a_col[:], in0=j_col[:], scalar1=CONSTANT, scalar2=-sum(WEIGHTS), op0=ALU.mult, op1=ALU.add)
+            nc.vector.tensor_scalar(out=minus_eps_j[:], in0=j_col[:], scalar1=-EPS, scalar2=None, op0=ALU.mult)
             for m in range(MODES):
                 nc.vector.tensor_scalar(out=c_rows[:, m, :], in0=zeros[:], scalar1=WEIGHTS[m], scalar2=None, op0=ALU.add)
 
@@ -153,11 +151,12 @@ def tile_evidentialhead_pb_kernel(tc, h_act_bytes, h_act_scale, W3, b3, out_0, o
         rs_of = [None] * GROUPS
         x_of = [None] * GROUPS
         xt_of = [None] * GROUPS
+        w_of = [None] * GROUPS
         e_of = {}
 
         def feed(g):
             turned_of, grouped_of, acc_of = {}, {}, {}
-            by_vector = GROUP if g == 0 else (LEAD if g <= 2 else 0)
+            by_vector = GROUP if g == 0 else (LEAD if g <= 2 else STEADY)
 
             def widen(s):
                 if s == 0:
@@ -308,6 +307,12 @@ def tile_evidentialhead_pb_kernel(tc, h_act_bytes, h_act_scale, W3, b3, out_0, o
                     dv = dst[:].rearrange("p (n two m) -> p n two m", two=2, m=d * GROUP)
                     first, second = sv[:, :, 0, :], sv[:, :, 1, :]
                     larger, smaller = dv[:, :, 0, :], dv[:, :, 1, :]
+                if n == 0:
+                    for h in range(QUADS):
+                        sel = slice(QUAD * h, QUAD * (h + 1))
+                        nc.vector.tensor_tensor(out=larger[:, :, sel], in0=first[:, :, sel], in1=second[:, :, sel], op=ALU.max)
+                        nc.vector.tensor_tensor(out=smaller[:, :, sel], in0=first[:, :, sel], in1=second[:, :, sel], op=ALU.min)
+                    return
                 runs = first.shape[1]
                 cut = parts if runs > 1 else 1
                 for part in range(cut):
@@ -352,7 +357,11 @@ def tile_evidentialhead_pb_kernel(tc, h_act_bytes, h_act_scale, W3, b3, out_0, o
                     nc.tensor.transpose(xt_ps[:, s, :], x_of[g][:, (QUAD * h + s) * C : (QUAD * h + s + 1) * C], ident[:])
                 if h == 0:
                     xt_of[g] = sortp.tile([P, GROUP, P], F32, name="xt_g", tag="xt", bufs=2)
-                nc.scalar.copy(out=xt_of[g][:, QUAD * h : QUAD * (h + 1), :], in_=xt_ps[:])
+                    w_of[g] = sortp.tile([P, GROUP, P], F32, name="w_g", tag="w", bufs=2)
+                tiles = slice(QUAD * h, QUAD * (h + 1))
+                nc.scalar.copy(out=xt_of[g][:, tiles, :], in_=xt_ps[:])
+                nc.scalar.activation(out=w_of[g][:, tiles, :], in_=xt_ps[:], func=ACT.Square, bias=half_eps_col[:])
+                nc.scalar.activation(out=w_of[g][:, tiles, :], in_=w_of[g][:, tiles, :], func=ACT.Copy, bias=-0.25 * EPS * EPS)
 
             return unit
 
@@ -372,9 +381,8 @@ def tile_evidentialhead_pb_kernel(tc, h_act_bytes, h_act_scale, W3, b3, out_0, o
                 if s % QUAD == 0:
                     g_of[(g, s // QUAD)] = psum_w.tile([P, QUAD, P], F32, name="g_q", tag="g_q")
                 g_turned = g_of[(g, s // QUAD)][:, s % QUAD, :]
-                nc.tensor.matmul(out=g_turned, lhsT=a_row[:], rhs=ident[:], is_transpose=True, start=True, stop=False)
                 for m in range(MODES):
-                    nc.tensor.matmul(out=g_turned, lhsT=y[:, m * C : (m + 1) * C], rhs=ident[:], is_transpose=True, start=False, stop=(m == MODES - 1))
+                    nc.tensor.matmul(out=g_turned, lhsT=y[:, m * C : (m + 1) * C], rhs=ident[:], is_transpose=True, start=(m == 0), stop=(m == MODES - 1))
 
             return unit
 
@@ -384,17 +392,15 @@ def tile_evidentialhead_pb_kernel(tc, h_act_bytes, h_act_scale, W3, b3, out_0, o
 
             def times_g():
                 kept["u"] = fin.tile([P, QUAD, P], F32, name="u_q", tag="u")
-                nc.vector.scalar_tensor_tensor(out=flat(kept["u"][:]), in0=flat(xt_of[g][:, QUAD * h : QUAD * (h + 1), :]), scalar=EPS, in1=flat(g_of[(g, h)][:]), op0=ALU.add, op1=ALU.mult)
-
-            def times_x():
-                nc.vector.scalar_tensor_tensor(out=flat(kept["u"][:]), in0=flat(kept["u"][:]), scalar=eps_j[:], in1=flat(xt_of[g][:, QUAD * h : QUAD * (h + 1), :]), op0=ALU.subtract, op1=ALU.mult)
+                nc.vector.scalar_tensor_tensor(out=flat(kept["u"][:]), in0=flat(g_of[(g, h)][:]), scalar=a_col[:], in1=flat(w_of[g][:, QUAD * h : QUAD * (h + 1), :]), op0=ALU.add, op1=ALU.mult)
                 for s in range(QUAD):
-                    nc.tensor.matmul(out=g_of[(g, h)][:, s, 0:1], lhsT=kept["u"][:, s, :], rhs=one_col[:], start=True, stop=True)
+                    nc.tensor.matmul(out=g_of[(g, h)][:, s, 0:1], lhsT=kept["u"][:, s, :], rhs=one_col[:], start=True, stop=False)
+                    nc.tensor.matmul(out=g_of[(g, h)][:, s, 0:1], lhsT=xt_of[g][:, QUAD * h + s, :], rhs=minus_eps_j[:], start=False, stop=True)
 
             def collect():
                 nc.vector.tensor_copy(out=dissonance[:, first : first + QUAD], in_=g_of[(g, h)][:, :, 0])
 
-            return [times_g, times_x, collect]
+            return [times_g, collect]
 
         def spread(units, start, end):
             return [(start + (end - start) * pos / max(len(units) - 1, 1), units[pos]) for pos in range(len(units))]
@@ -455,12 +461,12 @@ def tile_evidentialhead_pb_kernel(tc, h_act_bytes, h_act_scale, W3, b3, out_0, o
                 late = [scan(p, s) for s in range(early, GROUP)]
                 if early > QUAD:
                     first_quad = weigh(p, 0)
-                    marked += spread(first_quad[:2], scans[QUAD][0] + 0.03, scans[QUAD][0] + 0.08) + [(COLLECT_FIRST, first_quad[2])]
+                    marked += [(scans[QUAD][0] + 0.03, first_quad[0]), (COLLECT_FIRST, first_quad[1])]
                 else:
                     first_quad = weigh(p, 0)
-                    late = late[:LATE_SCANS] + [first_quad[0], late[LATE_SCANS], first_quad[1], late[LATE_SCANS + 1], first_quad[2]]
+                    late = late[:LATE_SCANS] + [first_quad[0]] + late[LATE_SCANS:] + [first_quad[1]]
                 second_quad = weigh(p, 1)
-                carried = spread(second_quad[:2], CARRY_FROM, CARRY_TO) + [(COLLECT_SECOND, second_quad[2])]
+                carried = [(CARRY_FROM, second_quad[0]), (COLLECT_SECOND, second_quad[1])]
             write(chain, marked)
         write(late, [])
         write([], carried)

@@ -54,10 +54,9 @@ TURN_FROM, TURN_TO = 0.05, 0.62
 QUANT_FROM, QUANT_TO = 0.38, 0.96
 POWERS_TO = 0.02
 SCANS_FROM, SCANS_TO = 0.16, 0.80
-STEADY = 1
 LEAD = 3
 ALPHA_FROM, PROB_FROM = 0.20, 0.62
-CARRY_FROM = 0.18
+CARRY_FROM, CARRY_TO = 0.18, 0.24
 COLLECT_FIRST, COLLECT_SECOND = 0.96, 0.55
 
 
@@ -102,6 +101,8 @@ def tile_evidentialhead_pb_kernel(tc, h_act_bytes, h_act_scale, W3, b3, out_0, o
         nc.gpsimd.memset(zeros[:], 0.0)
         ident = const.tile([P, P], F32, name="ident")
         make_identity(nc, ident[:])
+        index_i = const.tile([P, C], I32, name="index_i")
+        nc.gpsimd.iota(out=index_i[:], pattern=[[1, C]], base=0, channel_multiplier=0)
         partition_i = const.tile([P, 1], I32, name="partition_i")
         nc.gpsimd.iota(out=partition_i[:], pattern=[[0, 1]], base=0, channel_multiplier=1)
         lam = [const.tile([P, GROUP, C], F32, name="lam0"), const.tile([P, GROUP, C], F32, name="lam1")]
@@ -130,15 +131,16 @@ def tile_evidentialhead_pb_kernel(tc, h_act_bytes, h_act_scale, W3, b3, out_0, o
         half_eps_col = const.tile([P, 1], F32, name="half_eps_col")
         nc.vector.tensor_scalar(out=half_eps_col[:], in0=zeros[:, 0:1], scalar1=0.5 * EPS, scalar2=None, op0=ALU.add)
 
-        j_col = const.tile([P, 1], F32, name="j_col")
-        a_col = const.tile([P, 1], F32, name="a_col")
-        minus_eps_j = const.tile([P, 1], F32, name="minus_eps_j")
+        j_row = const.tile([P, C], F32, name="j_row")
+        a_row = const.tile([P, C], F32, name="a_row")
+        eps_j = const.tile([P, 1], F32, name="eps_j")
         c_rows = const.tile([P, MODES, C], F32, name="c_rows")
 
         def constants():
-            nc.vector.tensor_copy(out=j_col[:], in_=partition_i[:])
-            nc.vector.tensor_scalar(out=a_col[:], in0=j_col[:], scalar1=CONSTANT, scalar2=-sum(WEIGHTS), op0=ALU.mult, op1=ALU.add)
-            nc.vector.tensor_scalar(out=minus_eps_j[:], in0=j_col[:], scalar1=-EPS, scalar2=None, op0=ALU.mult)
+            nc.vector.tensor_copy(out=j_row[:], in_=index_i[:])
+            nc.vector.tensor_scalar(out=a_row[:], in0=j_row[:], scalar1=CONSTANT, scalar2=-sum(WEIGHTS), op0=ALU.mult, op1=ALU.add)
+            nc.vector.tensor_copy(out=eps_j[:], in_=partition_i[:])
+            nc.vector.tensor_scalar(out=eps_j[:], in0=eps_j[:], scalar1=EPS, scalar2=None, op0=ALU.mult)
             for m in range(MODES):
                 nc.vector.tensor_scalar(out=c_rows[:, m, :], in0=zeros[:], scalar1=WEIGHTS[m], scalar2=None, op0=ALU.add)
 
@@ -147,16 +149,14 @@ def tile_evidentialhead_pb_kernel(tc, h_act_bytes, h_act_scale, W3, b3, out_0, o
 
         logit_of = [None] * GROUPS
         soft_of = [None] * GROUPS
-        sorted_of = [None] * GROUPS
         rs_of = [None] * GROUPS
         x_of = [None] * GROUPS
         xt_of = [None] * GROUPS
-        w_of = [None] * GROUPS
         e_of = {}
 
         def feed(g):
             turned_of, grouped_of, acc_of = {}, {}, {}
-            by_vector = GROUP if g == 0 else (LEAD if g <= 2 else STEADY)
+            by_vector = GROUP if g == 0 else (LEAD if g <= 2 else 0)
 
             def widen(s):
                 if s == 0:
@@ -285,55 +285,52 @@ def tile_evidentialhead_pb_kernel(tc, h_act_bytes, h_act_scale, W3, b3, out_0, o
 
             return unit
 
-        def sort_stage(g, n, d, mirrored, parts):
+        def sort_stage(g, n, p, k):
             def unit():
                 if n == 0:
                     held[g]["even"] = sortp.tile([P, C * GROUP], F32, name="even_g", tag="even", bufs=1)
                     held[g]["odd"] = sortp.tile([P, C * GROUP], F32, name="odd_g", tag="odd", bufs=1)
                 dst = held[g]["even"] if n % 2 == 0 else held[g]["odd"]
                 src = held[g]["odd"] if n % 2 == 0 else held[g]["even"]
-                if n == 0:
-                    sv = held[g]["ev"][:].rearrange("p i (n two) -> p n two i", two=2)
-                    dv = dst[:].rearrange("p (n two i) -> p n two i", two=2, i=GROUP)
-                    first, second = sv[:, :, 0, :], sv[:, :, 1, :]
-                    larger, smaller = dv[:, :, 0, :], dv[:, :, 1, :]
-                elif mirrored:
-                    sv = src[:].rearrange("p (n two d i) -> p n two d i", two=2, d=d, i=GROUP)
-                    dv = dst[:].rearrange("p (n two d i) -> p n two d i", two=2, d=d, i=GROUP)
-                    first, second = sv[:, :, 0, :, :], sv[:, :, 1, ::-1, :]
-                    larger, smaller = dv[:, :, 0, :, :], dv[:, :, 1, :, :]
-                else:
-                    sv = src[:].rearrange("p (n two m) -> p n two m", two=2, m=d * GROUP)
-                    dv = dst[:].rearrange("p (n two m) -> p n two m", two=2, m=d * GROUP)
-                    first, second = sv[:, :, 0, :], sv[:, :, 1, :]
-                    larger, smaller = dv[:, :, 0, :], dv[:, :, 1, :]
-                if n == 0:
-                    for h in range(QUADS):
-                        sel = slice(QUAD * h, QUAD * (h + 1))
-                        nc.vector.tensor_tensor(out=larger[:, :, sel], in0=first[:, :, sel], in1=second[:, :, sel], op=ALU.max)
-                        nc.vector.tensor_tensor(out=smaller[:, :, sel], in0=first[:, :, sel], in1=second[:, :, sel], op=ALU.min)
-                    return
-                runs = first.shape[1]
-                cut = parts if runs > 1 else 1
-                for part in range(cut):
-                    sel = slice(part * runs // cut, (part + 1) * runs // cut)
-                    nc.vector.tensor_tensor(out=larger[:, sel], in0=first[:, sel], in1=second[:, sel], op=ALU.max)
-                    nc.vector.tensor_tensor(out=smaller[:, sel], in0=first[:, sel], in1=second[:, sel], op=ALU.min)
+                for h in range(QUADS):
+                    part = slice(h * C * QUAD, (h + 1) * C * QUAD)
+                    if n == 0:
+                        sv = held[g]["ev"][:, QUAD * h : QUAD * (h + 1), :].rearrange("p i (n two) -> p n two i", two=2)
+                        dv = dst[:, part].rearrange("p (n two i) -> p n two i", two=2, i=QUAD)
+                        first, second = sv[:, :, 0, :], sv[:, :, 1, :]
+                        larger, smaller = dv[:, :, 0, :], dv[:, :, 1, :]
+                    elif k == p:
+                        sv = src[:, part].rearrange("p (b two m) -> p b two m", two=2, m=p * QUAD)
+                        dv = dst[:, part].rearrange("p (b two m) -> p b two m", two=2, m=p * QUAD)
+                        first, second = sv[:, :, 0, :], sv[:, :, 1, :]
+                        larger, smaller = dv[:, :, 0, :], dv[:, :, 1, :]
+                    else:
+                        inner = slice(k * QUAD, (2 * p - k) * QUAD)
+                        sv = src[:, part].rearrange("p (b e) -> p b e", e=2 * p * QUAD)[:, :, inner].rearrange("p b (m two r) -> p b m two r", two=2, r=k * QUAD)
+                        dv = dst[:, part].rearrange("p (b e) -> p b e", e=2 * p * QUAD)[:, :, inner].rearrange("p b (m two r) -> p b m two r", two=2, r=k * QUAD)
+                        first, second = sv[:, :, :, 0, :], sv[:, :, :, 1, :]
+                        larger, smaller = dv[:, :, :, 0, :], dv[:, :, :, 1, :]
+                    nc.vector.tensor_tensor(out=larger, in0=first, in1=second, op=ALU.max)
+                    nc.vector.tensor_tensor(out=smaller, in0=first, in1=second, op=ALU.min)
+                if p >= 2 and k == p // 2:
+                    quarters_from = src[:].rearrange("p (b f r) -> p b f r", f=4, r=(p // 2) * QUAD)
+                    quarters_to = dst[:].rearrange("p (b f r) -> p b f r", f=4, r=(p // 2) * QUAD)
+                    nc.vector.tensor_copy(out=quarters_to[:, :, 0:4:3, :], in_=quarters_from[:, :, 0:4:3, :])
 
             return unit
 
-        def sort_chain(g, parts):
+        def sort_chain(g):
             units = []
-            for level in range(1, LEVELS + 1):
-                for step in range(level):
-                    d = (1 << level) >> (step + 1)
-                    units.append(sort_stage(g, len(units), d, step == 0 and d > 1, parts))
+            for level in range(LEVELS):
+                p = 1 << level
+                for step in range(level + 1):
+                    units.append(sort_stage(g, len(units), p, p >> step))
             return units
 
         def belief(g, s):
             if s == 0:
                 x_of[g] = sortp.tile([P, GROUP * C], F32, name="x_g", tag="x")
-            nc.scalar.activation(out=x_of[g][:, s * C : (s + 1) * C], in_=held[g]["odd"][:].rearrange("p (e i) -> p e i", i=GROUP)[:, :, s], func=ACT.Copy, scale=rs_of[g][:, s : s + 1])
+            nc.scalar.activation(out=x_of[g][:, s * C : (s + 1) * C], in_=held[g]["odd"][:].rearrange("p (h e i) -> p h i e", h=QUADS, i=QUAD)[:, s // QUAD, s % QUAD, :], func=ACT.Copy, scale=rs_of[g][:, s : s + 1])
 
         def ln_belief(g):
             held[g]["L"] = grp.tile([P, GROUP, C], F32, name="l_g", tag="L")
@@ -357,11 +354,7 @@ def tile_evidentialhead_pb_kernel(tc, h_act_bytes, h_act_scale, W3, b3, out_0, o
                     nc.tensor.transpose(xt_ps[:, s, :], x_of[g][:, (QUAD * h + s) * C : (QUAD * h + s + 1) * C], ident[:])
                 if h == 0:
                     xt_of[g] = sortp.tile([P, GROUP, P], F32, name="xt_g", tag="xt", bufs=2)
-                    w_of[g] = sortp.tile([P, GROUP, P], F32, name="w_g", tag="w", bufs=2)
-                tiles = slice(QUAD * h, QUAD * (h + 1))
-                nc.scalar.copy(out=xt_of[g][:, tiles, :], in_=xt_ps[:])
-                nc.scalar.activation(out=w_of[g][:, tiles, :], in_=xt_ps[:], func=ACT.Square, bias=half_eps_col[:])
-                nc.scalar.activation(out=w_of[g][:, tiles, :], in_=w_of[g][:, tiles, :], func=ACT.Copy, bias=-0.25 * EPS * EPS)
+                nc.scalar.copy(out=xt_of[g][:, QUAD * h : QUAD * (h + 1), :], in_=xt_ps[:])
 
             return unit
 
@@ -381,8 +374,9 @@ def tile_evidentialhead_pb_kernel(tc, h_act_bytes, h_act_scale, W3, b3, out_0, o
                 if s % QUAD == 0:
                     g_of[(g, s // QUAD)] = psum_w.tile([P, QUAD, P], F32, name="g_q", tag="g_q")
                 g_turned = g_of[(g, s // QUAD)][:, s % QUAD, :]
+                nc.tensor.matmul(out=g_turned, lhsT=a_row[:], rhs=ident[:], is_transpose=True, start=True, stop=False)
                 for m in range(MODES):
-                    nc.tensor.matmul(out=g_turned, lhsT=y[:, m * C : (m + 1) * C], rhs=ident[:], is_transpose=True, start=(m == 0), stop=(m == MODES - 1))
+                    nc.tensor.matmul(out=g_turned, lhsT=y[:, m * C : (m + 1) * C], rhs=ident[:], is_transpose=True, start=False, stop=(m == MODES - 1))
 
             return unit
 
@@ -392,15 +386,17 @@ def tile_evidentialhead_pb_kernel(tc, h_act_bytes, h_act_scale, W3, b3, out_0, o
 
             def times_g():
                 kept["u"] = fin.tile([P, QUAD, P], F32, name="u_q", tag="u")
-                nc.vector.scalar_tensor_tensor(out=flat(kept["u"][:]), in0=flat(g_of[(g, h)][:]), scalar=a_col[:], in1=flat(w_of[g][:, QUAD * h : QUAD * (h + 1), :]), op0=ALU.add, op1=ALU.mult)
+                nc.vector.scalar_tensor_tensor(out=flat(kept["u"][:]), in0=flat(xt_of[g][:, QUAD * h : QUAD * (h + 1), :]), scalar=EPS, in1=flat(g_of[(g, h)][:]), op0=ALU.add, op1=ALU.mult)
+
+            def times_x():
+                nc.vector.scalar_tensor_tensor(out=flat(kept["u"][:]), in0=flat(kept["u"][:]), scalar=eps_j[:], in1=flat(xt_of[g][:, QUAD * h : QUAD * (h + 1), :]), op0=ALU.subtract, op1=ALU.mult)
                 for s in range(QUAD):
-                    nc.tensor.matmul(out=g_of[(g, h)][:, s, 0:1], lhsT=kept["u"][:, s, :], rhs=one_col[:], start=True, stop=False)
-                    nc.tensor.matmul(out=g_of[(g, h)][:, s, 0:1], lhsT=xt_of[g][:, QUAD * h + s, :], rhs=minus_eps_j[:], start=False, stop=True)
+                    nc.tensor.matmul(out=g_of[(g, h)][:, s, 0:1], lhsT=kept["u"][:, s, :], rhs=one_col[:], start=True, stop=True)
 
             def collect():
                 nc.vector.tensor_copy(out=dissonance[:, first : first + QUAD], in_=g_of[(g, h)][:, :, 0])
 
-            return [times_g, collect]
+            return [times_g, times_x, collect]
 
         def spread(units, start, end):
             return [(start + (end - start) * pos / max(len(units) - 1, 1), units[pos]) for pos in range(len(units))]
@@ -448,7 +444,7 @@ def tile_evidentialhead_pb_kernel(tc, h_act_bytes, h_act_scale, W3, b3, out_0, o
                 marked += [(TURN_FROM + 0.1, weights)]
             late, carried, chain = [], [], []
             if 0 <= sorting < GROUPS:
-                chain = sort_chain(sorting, 2)
+                chain = sort_chain(sorting)
                 marked += spread([alpha(sorting, s) for s in range(GROUP)], ALPHA_FROM, ALPHA_FROM + 0.04)
                 marked += [(PROB_FROM - 0.05, reciprocal(sorting)), (PROB_FROM, vacuity_of(sorting))]
                 marked += spread([prob(sorting, s) for s in range(GROUP)], PROB_FROM, PROB_FROM + 0.04)
@@ -461,12 +457,12 @@ def tile_evidentialhead_pb_kernel(tc, h_act_bytes, h_act_scale, W3, b3, out_0, o
                 late = [scan(p, s) for s in range(early, GROUP)]
                 if early > QUAD:
                     first_quad = weigh(p, 0)
-                    marked += [(scans[QUAD][0] + 0.03, first_quad[0]), (COLLECT_FIRST, first_quad[1])]
+                    marked += spread(first_quad[:2], scans[QUAD][0] + 0.03, scans[QUAD][0] + 0.08) + [(COLLECT_FIRST, first_quad[2])]
                 else:
                     first_quad = weigh(p, 0)
-                    late = late[:LATE_SCANS] + [first_quad[0]] + late[LATE_SCANS:] + [first_quad[1]]
+                    late = late[:LATE_SCANS] + [first_quad[0], late[LATE_SCANS], first_quad[1], late[LATE_SCANS + 1], first_quad[2]]
                 second_quad = weigh(p, 1)
-                carried = [(CARRY_FROM, second_quad[0]), (COLLECT_SECOND, second_quad[1])]
+                carried = spread(second_quad[:2], CARRY_FROM, CARRY_TO) + [(COLLECT_SECOND, second_quad[2])]
             write(chain, marked)
         write(late, [])
         write([], carried)

@@ -118,13 +118,14 @@ def tile_evidentialhead_pb_kernel(tc, h_act_bytes, h_act_scale, W3, b3, out_0, o
         bias_rows = const.tile([P, C], F32, name="bias_rows")
         bias_col = const.tile([P, 1], F32, name="bias_col")
 
+        nc.scalar.copy(out=w_grouped[:], in_=w_raw[:].rearrange("p q j n -> p q n j"))
+        nc.scalar.copy(out=bias_rows[:], in_=bias_bc[:])
+        bias_turned = psum_back.tile([P, QUAD, P], F32, name="bias_turned", tag="back")
+        nc.tensor.transpose(bias_turned[:, 0, :], bias_rows[:], ident[:])
+        nc.scalar.copy(out=bias_col[:], in_=bias_turned[:, 0, 0:1])
+
         def weights():
-            nc.vector.tensor_copy(out=w_grouped[:], in_=w_raw[:].rearrange("p q j n -> p q n j"))
-            nc.vector.tensor_copy(out=bias_rows[:], in_=bias_bc[:])
-            bias_turned = psum_back.tile([P, QUAD, P], F32, name="bias_turned", tag="back")
-            nc.tensor.transpose(bias_turned[:, 0, :], bias_rows[:], ident[:])
             nc.vector.quantize_mx(out=w_codes[:].bitcast(FP8X4), scales=w_scales[:], in_=w_grouped[:].rearrange("p q n j -> p (q n j)"))
-            nc.vector.tensor_copy(out=bias_col[:], in_=bias_turned[:, 0, 0:1])
 
         one_col = const.tile([P, 1], F32, name="one_col")
         nc.vector.memset(one_col[:], 1.0)
@@ -271,7 +272,7 @@ def tile_evidentialhead_pb_kernel(tc, h_act_bytes, h_act_scale, W3, b3, out_0, o
 
         def vacuity_of(g):
             def unit():
-                nc.vector.tensor_scalar(out=vacuity[:, GROUP * g : GROUP * (g + 1)], in0=rs_of[g][:], scalar1=float(C), scalar2=None, op0=ALU.mult)
+                nc.scalar.activation(out=vacuity[:, GROUP * g : GROUP * (g + 1)], in_=rs_of[g][:], func=ACT.Copy, scale=float(C))
 
             return unit
 
@@ -312,10 +313,10 @@ def tile_evidentialhead_pb_kernel(tc, h_act_bytes, h_act_scale, W3, b3, out_0, o
                         larger, smaller = dv[:, :, :, 0, :], dv[:, :, :, 1, :]
                     nc.vector.tensor_tensor(out=larger, in0=first, in1=second, op=ALU.max)
                     nc.vector.tensor_tensor(out=smaller, in0=first, in1=second, op=ALU.min)
-                if p >= 2 and k == p // 2:
-                    quarters_from = src[:].rearrange("p (b f r) -> p b f r", f=4, r=(p // 2) * QUAD)
-                    quarters_to = dst[:].rearrange("p (b f r) -> p b f r", f=4, r=(p // 2) * QUAD)
-                    nc.vector.tensor_copy(out=quarters_to[:, :, 0:4:3, :], in_=quarters_from[:, :, 0:4:3, :])
+                    if h == 0 and p >= 2 and k == p // 2:
+                        quarters_from = src[:].rearrange("p (b f r) -> p b f r", f=4, r=(p // 2) * QUAD)
+                        quarters_to = dst[:].rearrange("p (b f r) -> p b f r", f=4, r=(p // 2) * QUAD)
+                        nc.vector.tensor_copy(out=quarters_to[:, :, 0:4:3, :], in_=quarters_from[:, :, 0:4:3, :])
 
             return unit
 

from contextlib import ExitStack

import concourse.mybir as mybir
from concourse.masks import make_identity

ROWS, K, C = 5120, 1024, 128
FLOPS = 2 * ROWS * K * C

F32 = mybir.dt.float32
BF16 = mybir.dt.bfloat16
I32 = mybir.dt.int32
U32 = mybir.dt.uint32
U8 = mybir.dt.uint8
FP8 = mybir.dt.float8_e4m3fn
FP8X4 = mybir.dt.float8_e4m3fn_x4
ACT = mybir.ActivationFunctionType
ALU = mybir.AluOpType
AX = mybir.AxisListType

P = 128
TILES = ROWS // P
QUAD = 4
GROUP = 8
GROUPS = TILES // GROUP
QUADS = GROUP // QUAD
PASSES = K // (4 * P)
WORDS = 2 * P
FIRST_LOAD = 2
LEVELS = 7
STAGES = LEVELS * (LEVELS + 1) // 2
EPS = 1e-8
CONSTANT = 1.99999999975556
EXPONENTS = (1.00000003251, 2.00018891269, 2.98310507162, 4.43669433027, 4.72915341974, 5.05369642201, 5.80774242344, 7.13256179473, 8.43355250839)
WEIGHTS = (-1.99999945329247, 2.00220339501363, -1.89071956839634, 10.7493049500827, -18.1703486275972, 9.20543703239164, -0.941251246893103, 0.0485658928379882, -0.00319237421115004)
MODES = len(EXPONENTS)
RESET = -10000.0


def fit_error(r):
    return abs(CONSTANT + sum(WEIGHTS[m] * r ** EXPONENTS[m] for m in range(MODES)) - 2.0 / (1.0 + r))


assert max(fit_error(i / 4096.0) for i in range(4097)) < 4e-10
assert max(fit_error(0.5 ** i) for i in range(12, 80)) < 4e-10


def flat(ap):
    return ap.rearrange("p t c -> p (t c)")


KEPT = 3
LATE_SCANS = 2
TURN_FROM, TURN_TO = 0.05, 0.62
QUANT_FROM, QUANT_TO = 0.38, 0.96
POWERS_TO = 0.02
SCANS_FROM, SCANS_TO = 0.16, 0.80
LEAD = 3
ALPHA_FROM, PROB_FROM = 0.20, 0.62
CARRY_FROM, CARRY_TO = 0.18, 0.24
COLLECT_FIRST, COLLECT_SECOND = 0.96, 0.55


def tile_evidentialhead_pb_kernel(tc, h_act_bytes, h_act_scale, W3, b3, out_0, out_1, out_2, out_3, out_4):
    nc = tc.nc
    with ExitStack() as ctx:
        ctx.enter_context(tc.manual_schedule())
        const = ctx.enter_context(tc.tile_pool(name="const", bufs=1))
        stage = ctx.enter_context(tc.tile_pool(name="stage", bufs=3))
        grp = ctx.enter_context(tc.tile_pool(name="grp", bufs=2))
        outp = ctx.enter_context(tc.tile_pool(name="outp", bufs=1))
        sortp = ctx.enter_context(tc.tile_pool(name="sortp", bufs=3))
        modes = ctx.enter_context(tc.tile_pool(name="modes", bufs=2))
        fin = ctx.enter_context(tc.tile_pool(name="fin", bufs=2))
        psum_t = ctx.enter_context(tc.psum_pool(name="psum_t", bufs=2))
        psum_acc = ctx.enter_context(tc.psum_pool(name="psum_acc", bufs=2))
        psum_w = ctx.enter_context(tc.psum_pool(name="psum_w", bufs=2))
        psum_back = ctx.enter_context(tc.psum_pool(name="psum_back", bufs=2))

        bytes_hbm = h_act_bytes.rearrange("(p t) k -> p t k", t=TILES)
        alpha_hbm = out_0.rearrange("(p t) c -> p t c", t=TILES)
        evidence_hbm = out_1.rearrange("(p t) c -> p t c", t=TILES)
        prob_hbm = out_2.rearrange("(p t) c -> p t c", t=TILES)
        vacuity_hbm = out_3.rearrange("(p t) -> p t", t=TILES)
        dissonance_hbm = out_4.rearrange("(p t) -> p t", t=TILES)

        hbytes = const.tile([P, TILES, K], U8, name="hbytes")
        scale_bc = const.tile([P, K], F32, name="scale_bc")
        scale_col = const.tile([P, PASSES, 4], F32, name="scale_col")
        w_raw = const.tile([P, PASSES, 4, C], BF16, name="w_raw")
        bias_bc = const.tile([P, C], BF16, name="bias_bc")
        nc.scalar.dma_start(out=scale_bc[:], in_=h_act_scale.rearrange("o k -> (o k)").partition_broadcast(P))
        nc.scalar.dma_start(out=scale_col[:], in_=h_act_scale.rearrange("o (q p t) -> p (o q) t", p=P, t=4))
        nc.sync.dma_start(out=hbytes[:, 0:FIRST_LOAD, :], in_=bytes_hbm[:, 0:FIRST_LOAD, :])
        nc.sync.dma_start(out=w_raw[:], in_=W3.rearrange("(q p j) n -> p q j n", p=P, j=4))
        nc.sync.dma_start(out=bias_bc[:], in_=b3.partition_broadcast(P))
        for t in range(FIRST_LOAD, TILES, QUAD):
            e = min(t + QUAD, TILES)
            nc.sync.dma_start(out=hbytes[:, t:e, :], in_=bytes_hbm[:, t:e, :])

        zeros = const.tile([P, C], F32, name="zeros")
        nc.gpsimd.memset(zeros[:], 0.0)
        ident = const.tile([P, P], F32, name="ident")
        make_identity(nc, ident[:])
        index_i = const.tile([P, C], I32, name="index_i")
        nc.gpsimd.iota(out=index_i[:], pattern=[[1, C]], base=0, channel_multiplier=0)
        partition_i = const.tile([P, 1], I32, name="partition_i")
        nc.gpsimd.iota(out=partition_i[:], pattern=[[0, 1]], base=0, channel_multiplier=1)
        lam = [const.tile([P, GROUP, C], F32, name="lam0"), const.tile([P, GROUP, C], F32, name="lam1")]
        for lam_tile in lam:
            nc.gpsimd.memset(lam_tile[:], RESET)

        warm = const.tile([P, 1], F32, name="warm")
        nc.scalar.activation(out=warm[:], in_=zeros[:, 0:1], func=ACT.Exp)

        w_grouped = const.tile([P, PASSES, C, 4], BF16, name="w_grouped", align_bytes=64)
        w_codes = const.tile([P, PASSES * C], U32, name="w_codes", align_bytes=64)
        w_scales = const.tile([P, PASSES * C], U8, name="w_scales", align_bytes=64)
        bias_rows = const.tile([P, C], F32, name="bias_rows")
        bias_col = const.tile([P, 1], F32, name="bias_col")

        nc.scalar.copy(out=w_grouped[:], in_=w_raw[:].rearrange("p q j n -> p q n j"))
        nc.scalar.copy(out=bias_rows[:], in_=bias_bc[:])
        bias_turned = psum_back.tile([P, QUAD, P], F32, name="bias_turned", tag="back")
        nc.tensor.transpose(bias_turned[:, 0, :], bias_rows[:], ident[:])
        nc.scalar.copy(out=bias_col[:], in_=bias_turned[:, 0, 0:1])

        def weights():
            nc.vector.quantize_mx(out=w_codes[:].bitcast(FP8X4), scales=w_scales[:], in_=w_grouped[:].rearrange("p q n j -> p (q n j)"))

        one_col = const.tile([P, 1], F32, name="one_col")
        nc.vector.memset(one_col[:], 1.0)
        half_eps_col = const.tile([P, 1], F32, name="half_eps_col")
        nc.vector.tensor_scalar(out=half_eps_col[:], in0=zeros[:, 0:1], scalar1=0.5 * EPS, scalar2=None, op0=ALU.add)

        j_row = const.tile([P, C], F32, name="j_row")
        a_row = const.tile([P, C], F32, name="a_row")
        eps_j = const.tile([P, 1], F32, name="eps_j")
        c_rows = const.tile([P, MODES, C], F32, name="c_rows")

        def constants():
            nc.vector.tensor_copy(out=j_row[:], in_=index_i[:])
            nc.vector.tensor_scalar(out=a_row[:], in0=j_row[:], scalar1=CONSTANT, scalar2=-sum(WEIGHTS), op0=ALU.mult, op1=ALU.add)
            nc.vector.tensor_copy(out=eps_j[:], in_=partition_i[:])
            nc.vector.tensor_scalar(out=eps_j[:], in0=eps_j[:], scalar1=EPS, scalar2=None, op0=ALU.mult)
            for m in range(MODES):
                nc.vector.tensor_scalar(out=c_rows[:, m, :], in0=zeros[:], scalar1=WEIGHTS[m], scalar2=None, op0=ALU.add)

        vacuity = const.tile([P, TILES], F32, name="vacuity")
        dissonance = const.tile([P, TILES], F32, name="dissonance")

        logit_of = [None] * GROUPS
        soft_of = [None] * GROUPS
        rs_of = [None] * GROUPS
        x_of = [None] * GROUPS
        xt_of = [None] * GROUPS
        e_of = {}

        def feed(g):
            turned_of, grouped_of, acc_of = {}, {}, {}
            by_vector = GROUP if g == 0 else (LEAD if g <= 2 else 0)

            def widen(s):
                if s == 0:
                    logit_of[g] = grp.tile([P, GROUP, C], F32, name="logit_g", tag="logit")
                    soft_of[g] = grp.tile([P, GROUP, C], F32, name="soft_g", tag="soft")
                h_bf = stage.tile([P, K], BF16, name="h_bf", tag="h_bf", align_bytes=64)
                if s < by_vector:
                    nc.vector.tensor_tensor(out=h_bf[:], in0=hbytes[:, GROUP * g + s, :].bitcast(FP8), in1=scale_bc[:], op=ALU.mult)
                else:
                    nc.scalar.copy(out=h_bf[:], in_=hbytes[:, GROUP * g + s, :].bitcast(FP8))
                words = h_bf[:].bitcast(F32)
                turned = psum_t.tile([P, PASSES, 2, P], F32, name="turned", tag="turned")
                for q in range(PASSES):
                    for u in range(2):
                        nc.tensor.transpose(turned[:, q, u, :], words[:, WORDS * q + u : WORDS * (q + 1) : 2], ident[:])
                turned_of[s] = turned

            def copy_out(s):
                grouped = stage.tile([P, PASSES, P, 4], BF16, name="grouped", tag="grouped", align_bytes=64, bufs=GROUP)
                if s < by_vector:
                    nc.scalar.copy(out=grouped[:].bitcast(F32), in_=turned_of[s][:].rearrange("p q u r -> p q r u"))
                else:
                    halves = turned_of[s][:].bitcast(BF16).rearrange("p q u (r e) -> p q u r e", e=2)
                    scaled = stage.tile([P, PASSES, 2, P, 2], BF16, name="scaled", tag="scaled")
                    for q in range(PASSES):
                        for u in range(2):
                            for e in range(2):
                                nc.scalar.activation(out=scaled[:, q, u, :, e], in_=halves[:, q, u, :, e], func=ACT.Copy, scale=scale_col[:, q, 2 * u + e : 2 * u + e + 1])
                    nc.scalar.copy(out=grouped[:].bitcast(F32), in_=scaled[:].rearrange("p q u r e -> p q u (r e)").bitcast(F32).rearrange("p q u r -> p q r u"))
                grouped_of[s] = grouped

            def quantise(s):
                codes = stage.tile([P, PASSES * P], U32, name="codes", tag="codes", align_bytes=64, bufs=5)
                scales = stage.tile([P, PASSES * P], U8, name="scales", tag="scales", align_bytes=64, bufs=5)
                nc.vector.quantize_mx(out=codes[:].bitcast(FP8X4), scales=scales[:], in_=grouped_of[s][:].rearrange("p q r t -> p (q r t)"))
                if s % QUAD == 0:
                    acc_of[s // QUAD] = psum_acc.tile([P, QUAD, C], F32, name="acc", tag="acc")
                for q in range(PASSES):
                    cols = slice(P * q, P * (q + 1))
                    nc.tensor.matmul_mx(
                        out=acc_of[s // QUAD][:, s % QUAD, :],
                        lhsT=w_codes[:, cols].bitcast(FP8X4),
                        lhsT_scale=w_scales[:, cols],
                        rhs=codes[:, cols].bitcast(FP8X4),
                        rhs_scale=scales[:, cols],
                        start=(q == 0),
                        stop=(q == PASSES - 1),
                    )

            def relu_abs_exp(h):
                tiles = slice(QUAD * h, QUAD * (h + 1))
                nc.scalar.activation(out=soft_of[g][:, tiles, :], in_=acc_of[h][:], func=ACT.Abs, bias=bias_col[:])
                nc.scalar.activation(out=logit_of[g][:, tiles, :], in_=acc_of[h][:], func=ACT.Relu, bias=bias_col[:])
                nc.scalar.activation(out=soft_of[g][:, tiles, :], in_=soft_of[g][:, tiles, :], func=ACT.Exp, scale=-1.0)

            def scalar_step(i):
                def unit():
                    if i < GROUP:
                        widen(i)
                    if i >= 1:
                        copy_out(i - 1)

                return unit

            def vector_step(i):
                def unit():
                    if i % QUAD == 0 and i > 0:
                        relu_abs_exp(i // QUAD - 1)
                    if i < GROUP:
                        quantise(i)

                return unit

            return [scalar_step(i) for i in range(GROUP + 1)], [vector_step(i) for i in range(GROUP + 1)]

        held = [dict() for g in range(GROUPS)]

        def ln_softplus(g):
            nc.scalar.activation(out=flat(soft_of[g][:]), in_=flat(soft_of[g][:]), func=ACT.Ln, bias=one_col[:])

        def evidence_turn(g, h):
            held[g][("ev_ps", h)] = psum_back.tile([P, QUAD, C], F32, name="ev_ps", tag="back")
            for s in range(QUAD):
                out = held[g][("ev_ps", h)][:, s, :]
                nc.tensor.matmul(out=out, lhsT=logit_of[g][:, QUAD * h + s, :], rhs=ident[:], is_transpose=True, start=True, stop=False)
                nc.tensor.matmul(out=out, lhsT=soft_of[g][:, QUAD * h + s, :], rhs=ident[:], is_transpose=True, start=False, stop=True)

        def evidence_copy(g, h):
            if h == 0:
                held[g]["ev"] = outp.tile([P, GROUP, C], F32, name="ev_g", tag="ev")
            nc.scalar.copy(out=held[g]["ev"][:, QUAD * h : QUAD * (h + 1), :], in_=held[g][("ev_ps", h)][:])
            if h == QUADS - 1:
                nc.sync.dma_start(out=evidence_hbm[:, GROUP * g : GROUP * (g + 1), :], in_=held[g]["ev"][:])

        def alpha(g, s):
            def unit():
                if s == 0:
                    held[g]["al"] = outp.tile([P, GROUP, C], F32, name="al_g", tag="al")
                    held[g]["S"] = fin.tile([P, GROUP], F32, name="s_g", tag="S")
                nc.scalar.activation(out=held[g]["al"][:, s, :], in_=held[g]["ev"][:, s, :], func=ACT.Identity, bias=one_col[:], accum_out=held[g]["S"][:, s : s + 1])
                if s == GROUP - 1:
                    nc.sync.dma_start(out=alpha_hbm[:, GROUP * g : GROUP * (g + 1), :], in_=held[g]["al"][:])

            return unit

        def reciprocal(g):
            def unit():
                rs_of[g] = fin.tile([P, GROUP], F32, name="rs_g", tag="rS")
                nc.vector.reciprocal(out=rs_of[g][:], in_=held[g]["S"][:])

            return unit

        def vacuity_of(g):
            def unit():
                nc.scalar.activation(out=vacuity[:, GROUP * g : GROUP * (g + 1)], in_=rs_of[g][:], func=ACT.Copy, scale=float(C))

            return unit

        def prob(g, s):
            def unit():
                if s == 0:
                    held[g]["pr"] = outp.tile([P, GROUP, C], F32, name="pr_g", tag="pr")
                nc.scalar.activation(out=held[g]["pr"][:, s, :], in_=held[g]["al"][:, s, :], func=ACT.Copy, scale=rs_of[g][:, s : s + 1])
                if s == GROUP - 1:
                    nc.sync.dma_start(out=prob_hbm[:, GROUP * g : GROUP * (g + 1), :], in_=held[g]["pr"][:])

            return unit

        def sort_stage(g, n, p, k):
            def unit():
                if n == 0:
                    held[g]["even"] = sortp.tile([P, C * GROUP], F32, name="even_g", tag="even", bufs=1)
                    held[g]["odd"] = sortp.tile([P, C * GROUP], F32, name="odd_g", tag="odd", bufs=1)
                dst = held[g]["even"] if n % 2 == 0 else held[g]["odd"]
                src = held[g]["odd"] if n % 2 == 0 else held[g]["even"]
                for h in range(QUADS):
                    part = slice(h * C * QUAD, (h + 1) * C * QUAD)
                    if n == 0:
                        sv = held[g]["ev"][:, QUAD * h : QUAD * (h + 1), :].rearrange("p i (n two) -> p n two i", two=2)
                        dv = dst[:, part].rearrange("p (n two i) -> p n two i", two=2, i=QUAD)
                        first, second = sv[:, :, 0, :], sv[:, :, 1, :]
                        larger, smaller = dv[:, :, 0, :], dv[:, :, 1, :]
                    elif k == p:
                        sv = src[:, part].rearrange("p (b two m) -> p b two m", two=2, m=p * QUAD)
                        dv = dst[:, part].rearrange("p (b two m) -> p b two m", two=2, m=p * QUAD)
                        first, second = sv[:, :, 0, :], sv[:, :, 1, :]
                        larger, smaller = dv[:, :, 0, :], dv[:, :, 1, :]
                    else:
                        inner = slice(k * QUAD, (2 * p - k) * QUAD)
                        sv = src[:, part].rearrange("p (b e) -> p b e", e=2 * p * QUAD)[:, :, inner].rearrange("p b (m two r) -> p b m two r", two=2, r=k * QUAD)
                        dv = dst[:, part].rearrange("p (b e) -> p b e", e=2 * p * QUAD)[:, :, inner].rearrange("p b (m two r) -> p b m two r", two=2, r=k * QUAD)
                        first, second = sv[:, :, :, 0, :], sv[:, :, :, 1, :]
                        larger, smaller = dv[:, :, :, 0, :], dv[:, :, :, 1, :]
                    nc.vector.tensor_tensor(out=larger, in0=first, in1=second, op=ALU.max)
                    nc.vector.tensor_tensor(out=smaller, in0=first, in1=second, op=ALU.min)
                    if h == 0 and p >= 2 and k == p // 2:
                        quarters_from = src[:].rearrange("p (b f r) -> p b f r", f=4, r=(p // 2) * QUAD)
                        quarters_to = dst[:].rearrange("p (b f r) -> p b f r", f=4, r=(p // 2) * QUAD)
                        nc.vector.tensor_copy(out=quarters_to[:, :, 0:4:3, :], in_=quarters_from[:, :, 0:4:3, :])

            return unit

        def sort_chain(g):
            units = []
            for level in range(LEVELS):
                p = 1 << level
                for step in range(level + 1):
                    units.append(sort_stage(g, len(units), p, p >> step))
            return units

        def belief(g, s):
            if s == 0:
                x_of[g] = sortp.tile([P, GROUP * C], F32, name="x_g", tag="x")
            nc.scalar.activation(out=x_of[g][:, s * C : (s + 1) * C], in_=held[g]["odd"][:].rearrange("p (h e i) -> p h i e", h=QUADS, i=QUAD)[:, s // QUAD, s % QUAD, :], func=ACT.Copy, scale=rs_of[g][:, s : s + 1])

        def ln_belief(g):
            held[g]["L"] = grp.tile([P, GROUP, C], F32, name="l_g", tag="L")
            nc.scalar.activation(out=flat(held[g]["L"][:]), in_=x_of[g][:], func=ACT.Ln, bias=half_eps_col[:])

        def steps_of_l(g):
            nc.vector.tensor_tensor(out=lam[g % 2][:, :, 1:C], in0=held[g]["L"][:, :, 1:C], in1=held[g]["L"][:, :, 0 : C - 1], op=ALU.subtract)

        def power(g, h, m):
            def unit():
                if m == 0:
                    e_of[(g, h)] = modes.tile([P, QUAD, MODES, C], F32, name="e_q", tag="e")
                nc.scalar.activation(out=e_of[(g, h)][:, :, m, :], in_=lam[g % 2][:, QUAD * h : QUAD * (h + 1), :], func=ACT.Exp, scale=EXPONENTS[m])

            return unit

        def turn_beliefs(g, h):
            def unit():
                xt_ps = psum_back.tile([P, QUAD, P], F32, name="xt_ps", tag="back")
                for s in range(QUAD):
                    nc.tensor.transpose(xt_ps[:, s, :], x_of[g][:, (QUAD * h + s) * C : (QUAD * h + s + 1) * C], ident[:])
                if h == 0:
                    xt_of[g] = sortp.tile([P, GROUP, P], F32, name="xt_g", tag="xt", bufs=2)
                nc.scalar.copy(out=xt_of[g][:, QUAD * h : QUAD * (h + 1), :], in_=xt_ps[:])

            return unit

        g_of = {}

        def scan(g, s):
            def unit():
                y = modes.tile([P, MODES * C], F32, name="y_t", tag="y", bufs=4)
                nc.vector.tensor_tensor_scan(
                    out=y[:],
                    data0=e_of[(g, s // QUAD)][:, s % QUAD, :, :].rearrange("p k j -> p (k j)"),
                    data1=c_rows[:].rearrange("p k j -> p (k j)"),
                    initial=0.0,
                    op0=ALU.mult,
                    op1=ALU.add,
                )
                if s % QUAD == 0:
                    g_of[(g, s // QUAD)] = psum_w.tile([P, QUAD, P], F32, name="g_q", tag="g_q")
                g_turned = g_of[(g, s // QUAD)][:, s % QUAD, :]
                nc.tensor.matmul(out=g_turned, lhsT=a_row[:], rhs=ident[:], is_transpose=True, start=True, stop=False)
                for m in range(MODES):
                    nc.tensor.matmul(out=g_turned, lhsT=y[:, m * C : (m + 1) * C], rhs=ident[:], is_transpose=True, start=False, stop=(m == MODES - 1))

            return unit

        def weigh(g, h):
            kept = {}
            first = GROUP * g + QUAD * h

            def times_g():
                kept["u"] = fin.tile([P, QUAD, P], F32, name="u_q", tag="u")
                nc.vector.scalar_tensor_tensor(out=flat(kept["u"][:]), in0=flat(xt_of[g][:, QUAD * h : QUAD * (h + 1), :]), scalar=EPS, in1=flat(g_of[(g, h)][:]), op0=ALU.add, op1=ALU.mult)

            def times_x():
                nc.vector.scalar_tensor_tensor(out=flat(kept["u"][:]), in0=flat(kept["u"][:]), scalar=eps_j[:], in1=flat(xt_of[g][:, QUAD * h : QUAD * (h + 1), :]), op0=ALU.subtract, op1=ALU.mult)
                for s in range(QUAD):
                    nc.tensor.matmul(out=g_of[(g, h)][:, s, 0:1], lhsT=kept["u"][:, s, :], rhs=one_col[:], start=True, stop=True)

            def collect():
                nc.vector.tensor_copy(out=dissonance[:, first : first + QUAD], in_=g_of[(g, h)][:, :, 0])

            return [times_g, times_x, collect]

        def spread(units, start, end):
            return [(start + (end - start) * pos / max(len(units) - 1, 1), units[pos]) for pos in range(len(units))]

        def write(chain, marked):
            marked = sorted(marked, key=lambda pair: pair[0])
            due = 0
            for pos in range(len(chain)):
                chain[pos]()
                while due < len(marked) and marked[due][0] * len(chain) <= pos + 1:
                    marked[due][1]()
                    due += 1
            for pair in marked[due:]:
                pair[1]()

        late = []
        carried = []
        for p in range(-2, GROUPS):
            sorting, feeding = p + 1, p + 2
            if 0 <= sorting < GROUPS:
                ln_softplus(sorting)
                for h in range(QUADS):
                    evidence_turn(sorting, h)
            if p >= 0:
                for s in range(GROUP):
                    belief(p, s)
                ln_belief(p)
            if 0 <= sorting < GROUPS:
                for h in range(QUADS):
                    evidence_copy(sorting, h)
            turn_units, quant_units = feed(feeding) if feeding < GROUPS else ([], [])
            if p >= -1 and not late:
                late = turn_units[:LEAD]
                turn_units = turn_units[LEAD:]
            for unit in late[:LATE_SCANS]:
                unit()
            if p == -1:
                constants()
            if p >= 0:
                steps_of_l(p)
            for unit in late[LATE_SCANS:]:
                unit()
            marked = carried + spread(turn_units, TURN_FROM, TURN_TO) + spread(quant_units, QUANT_FROM, QUANT_TO)
            if p == -2:
                marked += [(TURN_FROM + 0.1, weights)]
            late, carried, chain = [], [], []
            if 0 <= sorting < GROUPS:
                chain = sort_chain(sorting)
                marked += spread([alpha(sorting, s) for s in range(GROUP)], ALPHA_FROM, ALPHA_FROM + 0.04)
                marked += [(PROB_FROM - 0.05, reciprocal(sorting)), (PROB_FROM, vacuity_of(sorting))]
                marked += spread([prob(sorting, s) for s in range(GROUP)], PROB_FROM, PROB_FROM + 0.04)
            if p >= 0:
                marked += spread([power(p, h, m) for h in range(QUADS) for m in range(MODES)], 0.0, POWERS_TO)
                early = GROUP - (KEPT if sorting < GROUPS - 1 else QUAD)
                scans = spread([scan(p, s) for s in range(early)], SCANS_FROM, SCANS_TO)
                marked += scans
                marked += spread([turn_beliefs(p, h) for h in range(QUADS)], POWERS_TO + 0.01, POWERS_TO + 0.02)
                late = [scan(p, s) for s in range(early, GROUP)]
                if early > QUAD:
                    first_quad = weigh(p, 0)
                    marked += spread(first_quad[:2], scans[QUAD][0] + 0.03, scans[QUAD][0] + 0.08) + [(COLLECT_FIRST, first_quad[2])]
                else:
                    first_quad = weigh(p, 0)
                    late = late[:LATE_SCANS] + [first_quad[0], late[LATE_SCANS], first_quad[1], late[LATE_SCANS + 1], first_quad[2]]
                second_quad = weigh(p, 1)
                carried = spread(second_quad[:2], CARRY_FROM, CARRY_TO) + [(COLLECT_SECOND, second_quad[2])]
            write(chain, marked)
        write(late, [])
        write([], carried)
        nc.sync.dma_start(out=vacuity_hbm, in_=vacuity[:])
        nc.sync.dma_start(out=dissonance_hbm, in_=dissonance[:])
